import numpy as np
import ml_dtypes


def mxq(x, axis, fmt="e4m3"):
    dtype, down = {"e4m3": (ml_dtypes.float8_e4m3fn, 7), "e5m2": (ml_dtypes.float8_e5m2, 14)}[fmt]
    v = np.moveaxis(np.asarray(x, np.float32).astype(ml_dtypes.bfloat16).astype(np.float64), axis, -1)
    blocks = v.reshape(v.shape[:-1] + (-1, 32))
    amax = np.abs(blocks).max(-1, keepdims=True)
    byte = np.maximum(np.where(amax > 0, np.frexp(amax)[1] - 1 + 127, 0) - down, 1)
    scale = np.exp2(byte - 127.0)
    codes = (blocks / scale).astype(np.float32).astype(dtype).astype(np.float64)
    return np.moveaxis((codes * scale).reshape(v.shape), -1, axis)


WIDE = False


def mx_kscale(k):
    if not WIDE:
        return np.ones(k)
    levels = np.array([10, -10, 5, -5, 0])
    a = np.random.permutation(np.resize(levels, k // 512 * 4)).reshape(k // 512, 4)
    idx = np.arange(k)
    return np.exp2(a[idx // 512, idx % 128 // 32])


BF16 = ml_dtypes.bfloat16


def bf(x):
    return np.asarray(x, np.float32).astype(BF16)


def f64(x):
    return np.asarray(x).astype(np.float64)


T, N, D, E, OUT = 4, 512, 512, 2, 64
H0 = 2 * OUT
C = (E + 1) * D
EPS = 1e-12
SLOPE = 0.01


def leaky_relu(v):
    return np.where(v >= 0.0, v, SLOPE * v)


def setup_inputs():
    u = mx_kscale(D)
    cls = np.where(np.random.random((T, N)) < 0.5, -1.0, 1.0)
    pat = np.where(np.random.random((T, 1, D)) < 0.5, -1.0, 1.0)
    node_feat = (1.0 + 0.6 * cls[:, :, None] * pat + 0.4 * np.random.standard_normal((T, N, D))) * u
    same = cls[:, None, :, None] * cls[:, None, None, :]
    chan = ((-1.0) ** np.arange(E))[None, :, None, None]
    edge_feat = (0.5 + 0.5 * np.random.random((T, E, N, N))) * (1.0 + 0.6 * chan * same)
    edge_feat = edge_feat * np.where(np.random.random((T, E, N, N)) < 0.05, -1.0, 1.0)
    edge_feat = edge_feat * (np.random.random((T, E, N, 1)) >= 0.05) + 0.1 * N * np.eye(N)
    w0 = np.random.standard_normal((H0, C)) / np.sqrt(C) / np.tile(u, E + 1)
    return {"node_feat": bf(node_feat), "edge_feat": bf(edge_feat), "w0": bf(w0)}


def reference(node_feat, edge_feat, w0):
    nf = f64(node_feat)
    masked = f64(edge_feat) * (1.0 - np.eye(N))
    denom = np.maximum(np.abs(masked).sum(-1, keepdims=True), EPS)
    norm_edge = masked / denom
    aggr = mxq(norm_edge, 3, "e4m3") @ mxq(nf, 1, "e4m3")[:, None]
    x = np.concatenate([nf, aggr.transpose(0, 2, 1, 3).reshape(T, N, E * D)], axis=-1)
    return leaky_relu(mxq(x, 2, "e4m3") @ mxq(f64(w0), 1, "e4m3").T)

@@ -1,0 +1,184 @@
+from contextlib import ExitStack
+
+import concourse.mybir as mybir
+from concourse.masks import make_identity
+
+F32 = mybir.dt.float32
+BF16 = mybir.dt.bfloat16
+U32 = mybir.dt.uint32
+U8 = mybir.dt.uint8
+FP8X4 = mybir.dt.float8_e4m3fn_x4
+ALU = mybir.AluOpType
+ACT = mybir.ActivationFunctionType
+
+P = 128
+PACK = 4
+GRAPHS, CHANNELS, NODES, FEATURES, OUT_WIDTH = 4, 2, 512, 512, 128
+NODE_TILES = NODES // P
+FEATURE_TILES = FEATURES // P
+X_PASSES = 1 + CHANNELS
+EPS = 1e-12
+SLOPE = 0.01
+
+FLOPS = 2 * GRAPHS * CHANNELS * NODES * NODES * FEATURES + 2 * GRAPHS * NODES * X_PASSES * FEATURES * OUT_WIDTH
+
+
+def tile_nodeupdatenetwork_pa_kernel(tc, node_feat, edge_feat, w0, out):
+    nc = tc.nc
+    with ExitStack() as ctx:
+        consts = ctx.enter_context(tc.tile_pool(name="consts", bufs=1))
+        inputs = ctx.enter_context(tc.tile_pool(name="inputs", bufs=GRAPHS))
+        work = ctx.enter_context(tc.tile_pool(name="work", bufs=2))
+        scratch = ctx.enter_context(tc.tile_pool(name="scratch", bufs=4))
+        word_psum = ctx.enter_context(tc.psum_pool(name="word_psum", bufs=3))
+        aggr_psum = ctx.enter_context(tc.psum_pool(name="aggr_psum", bufs=3))
+        out_psum = ctx.enter_context(tc.psum_pool(name="out_psum", bufs=2))
+
+        edge_rows, feat_by_pair, feat_rows = [], [], []
+        w0_rows = consts.tile([P, X_PASSES * FEATURES], BF16)
+        for t in range(GRAPHS):
+            edges = inputs.tile([P, CHANNELS * NODE_TILES, NODES], BF16, name="edges")
+            nc.sync.dma_start(out=edges[:], in_=edge_feat[t].rearrange("e (i p) m -> p (e i) m", p=P))
+            edge_rows.append(edges[:].rearrange("p (e i) m -> p e i m", e=CHANNELS))
+            by_pair = inputs.tile([P, PACK, FEATURES], BF16, name="by_pair")
+            nc.sync.dma_start(
+                out=by_pair[:].rearrange("p (u e) d -> p u (e d)", u=2),
+                in_=node_feat[t].rearrange("(u p e) d -> p u (e d)", u=2, e=2),
+            )
+            feat_by_pair.append(by_pair)
+            rows = inputs.tile([P, NODE_TILES, FEATURES], BF16, name="rows")
+            nc.sync.dma_start(out=rows[:], in_=node_feat[t].rearrange("(i p) d -> p i d", p=P))
+            feat_rows.append(rows)
+            if t == 0:
+                nc.sync.dma_start(out=w0_rows[:], in_=w0)
+
+        ident_f32 = consts.tile([P, P], F32)
+        make_identity(nc, ident_f32[:])
+        ident_bf16 = consts.tile([P, P], BF16)
+        make_identity(nc, ident_bf16[:])
+        off_diagonal = consts.tile([P, P], BF16)
+        nc.vector.tensor_scalar(
+            out=off_diagonal[:], in0=ident_bf16[:], scalar1=-1.0, scalar2=1.0, op0=ALU.mult, op1=ALU.add
+        )
+
+        def quantise(grouped, codes, scales):
+            nc.vector.quantize_mx(out=codes.bitcast(FP8X4), scales=scales, in_=grouped)
+
+        def to_pair_order(matrix_rows, grouped, copy):
+            words = grouped.bitcast(F32).rearrange("p (r u) -> p r u", u=2)
+            for half in range(2):
+                bank = word_psum.tile([P, 2, 2 * P], F32, name="bank")
+                for i in range(2):
+                    row_words = matrix_rows[:, 2 * half + i, :].bitcast(F32)
+                    for u in range(2):
+                        nc.tensor.transpose(
+                            bank[:, u, i * P : (i + 1) * P], row_words[:, u * P : (u + 1) * P], ident_f32[:]
+                        )
+                copy(out=words[:, half * 2 * P : (half + 1) * 2 * P, :], in_=bank[:].rearrange("p u r -> p r u"))
+
+        w0_grouped = consts.tile([P, X_PASSES, PACK * OUT_WIDTH], BF16, align_bytes=64)
+        w0_codes = consts.tile([P, X_PASSES, OUT_WIDTH], U32, align_bytes=64)
+        w0_scales = consts.tile([P, X_PASSES, OUT_WIDTH], U8, align_bytes=64)
+        w0_words = word_psum.tile([P, 2, P], F32, name="bank")
+        for u in range(2):
+            nc.tensor.transpose(w0_words[:, u, :], w0_rows[:].bitcast(F32)[:, u * P : (u + 1) * P], ident_f32[:])
+        nc.vector.tensor_copy(
+            out=w0_grouped[:, 0, :].bitcast(F32).rearrange("p (h u) -> p h u", u=2),
+            in_=w0_words[:].rearrange("p u h -> p h u"),
+        )
+        for g in range(1, X_PASSES):
+            w0_tiles = word_psum.tile([P, FEATURE_TILES, P], BF16, name="bank")
+            for j in range(FEATURE_TILES):
+                first = g * FEATURES + j * P
+                nc.tensor.transpose(w0_tiles[:, j, :], w0_rows[:, first : first + P], ident_bf16[:])
+            nc.vector.tensor_copy(
+                out=w0_grouped[:, g, :].rearrange("p (h j) -> p h j", j=PACK),
+                in_=w0_tiles[:].rearrange("p j h -> p h j"),
+            )
+        for g in range(X_PASSES):
+            quantise(w0_grouped[:, g, :], w0_codes[:, g, :], w0_scales[:, g, :])
+
+        for t in range(GRAPHS):
+            feat_grouped = work.tile([P, PACK * FEATURES], BF16, align_bytes=64)
+            nc.vector.tensor_copy(
+                out=feat_grouped[:].rearrange("p (c i v) -> p c v i", i=4, v=PACK),
+                in_=feat_by_pair[t][:].rearrange("p v (c i) -> p c v i", i=4),
+            )
+            feat_codes = work.tile([P, FEATURES], U32, align_bytes=64)
+            feat_scales = work.tile([P, FEATURES], U8, align_bytes=64)
+            quantise(feat_grouped[:], feat_codes[:], feat_scales[:])
+
+            x_codes = work.tile([P, X_PASSES, NODES], U32, align_bytes=64)
+            x_scales = work.tile([P, X_PASSES, NODES], U8, align_bytes=64)
+            x0_grouped = work.tile([P, PACK * NODES], BF16, align_bytes=64)
+            to_pair_order(feat_rows[t], x0_grouped[:], nc.scalar.copy)
+            quantise(x0_grouped[:], x_codes[:, 0, :], x_scales[:, 0, :])
+
+            masked = edge_rows[t]
+            for i in range(NODE_TILES):
+                block = masked[:, :, i, i * P : (i + 1) * P]
+                nc.vector.tensor_tensor(
+                    out=block, in0=block, in1=off_diagonal[:].unsqueeze(1).to_broadcast([P, CHANNELS, P]), op=ALU.mult
+                )
+
+            for e in range(CHANNELS):
+                denom = work.tile([P, NODE_TILES], F32)
+                for i in range(NODE_TILES):
+                    absolute = scratch.tile([P, NODES], BF16)
+                    nc.scalar.activation(
+                        out=absolute[:], in_=masked[:, e, i, :], func=ACT.Abs, accum_out=denom[:, i : i + 1]
+                    )
+                inverse = work.tile([P, NODE_TILES], F32)
+                nc.vector.tensor_scalar_max(out=inverse[:], in0=denom[:], scalar1=EPS)
+                nc.vector.reciprocal(out=inverse[:], in_=inverse[:])
+                norm_edge = work.tile([P, NODE_TILES, NODES], BF16)
+                for i in range(NODE_TILES):
+                    nc.vector.tensor_scalar(
+                        out=norm_edge[:, i, :], in0=masked[:, e, i, :], scalar1=inverse[:, i : i + 1], scalar2=None,
+                        op0=ALU.mult,
+                    )
+
+                edge_grouped = work.tile([P, PACK * NODES], BF16, align_bytes=64)
+                to_pair_order(norm_edge, edge_grouped[:], nc.vector.tensor_copy)
+                edge_codes = work.tile([P, NODES], U32, align_bytes=64)
+                edge_scales = work.tile([P, NODES], U8, align_bytes=64)
+                quantise(edge_grouped[:], edge_codes[:], edge_scales[:])
+
+                aggr_grouped = work.tile([P, NODES, PACK], BF16, align_bytes=64)
+                for i in range(NODE_TILES):
+                    nodes = slice(i * P, (i + 1) * P)
+                    aggr_bank = aggr_psum.tile([P, FEATURE_TILES, P], F32)
+                    for j in range(FEATURE_TILES):
+                        features = slice(j * P, (j + 1) * P)
+                        nc.tensor.matmul_mx(
+                            out=aggr_bank[:, j, :],
+                            lhsT=feat_codes[:, features].bitcast(FP8X4),
+                            lhsT_scale=feat_scales[:, features],
+                            rhs=edge_codes[:, nodes].bitcast(FP8X4),
+                            rhs_scale=edge_scales[:, nodes],
+                            start=True,
+                            stop=True,
+                        )
+                    nc.scalar.copy(out=aggr_grouped[:, nodes, :], in_=aggr_bank[:].rearrange("p j n -> p n j"))
+                quantise(
+                    aggr_grouped[:].rearrange("p n j -> p (n j)"), x_codes[:, 1 + e, :], x_scales[:, 1 + e, :]
+                )
+
+            out_bank = out_psum.tile([P, NODE_TILES, OUT_WIDTH], F32)
+            for i in range(NODE_TILES):
+                nodes = slice(i * P, (i + 1) * P)
+                for g in range(X_PASSES):
+                    nc.tensor.matmul_mx(
+                        out=out_bank[:, i, :],
+                        lhsT=x_codes[:, g, nodes].bitcast(FP8X4),
+                        lhsT_scale=x_scales[:, g, nodes],
+                        rhs=w0_codes[:, g, :].bitcast(FP8X4),
+                        rhs_scale=w0_scales[:, g, :],
+                        start=(g == 0),
+                        stop=(g == X_PASSES - 1),
+                    )
+            sloped = work.tile([P, NODE_TILES, OUT_WIDTH], F32)
+            nc.scalar.activation(out=sloped[:], in_=out_bank[:], func=ACT.Copy, scale=SLOPE)
+            result = work.tile([P, NODE_TILES, OUT_WIDTH], F32)
+            nc.vector.tensor_tensor(out=result[:], in0=out_bank[:], in1=sloped[:], op=ALU.max)
+            nc.sync.dma_start(out=out[t].rearrange("(i p) h -> p i h", p=P), in_=result[:])

@@ -20,35 +20,45 @@ X_PASSES = 1 + CHANNELS
 EPS = 1e-12
 SLOPE = 0.01
 
+W0_STEP = -1
+
 FLOPS = 2 * GRAPHS * CHANNELS * NODES * NODES * FEATURES + 2 * GRAPHS * NODES * X_PASSES * FEATURES * OUT_WIDTH
+
+
+UNITS = GRAPHS * CHANNELS
+HALVES = 2
 
 
 def tile_nodeupdatenetwork_pa_kernel(tc, node_feat, edge_feat, w0, out):
     nc = tc.nc
     with ExitStack() as ctx:
         consts = ctx.enter_context(tc.tile_pool(name="consts", bufs=1))
-        inputs = ctx.enter_context(tc.tile_pool(name="inputs", bufs=GRAPHS))
+        edge_pool = ctx.enter_context(tc.tile_pool(name="edge_pool", bufs=UNITS))
+        feat_pool = ctx.enter_context(tc.tile_pool(name="feat_pool", bufs=GRAPHS))
         work = ctx.enter_context(tc.tile_pool(name="work", bufs=2))
         scratch = ctx.enter_context(tc.tile_pool(name="scratch", bufs=4))
         word_psum = ctx.enter_context(tc.psum_pool(name="word_psum", bufs=3))
-        aggr_psum = ctx.enter_context(tc.psum_pool(name="aggr_psum", bufs=3))
-        out_psum = ctx.enter_context(tc.psum_pool(name="out_psum", bufs=2))
+        aggr_psum = ctx.enter_context(tc.psum_pool(name="aggr_psum", bufs=NODE_TILES))
+        out_psum = ctx.enter_context(tc.psum_pool(name="out_psum", bufs=1))
+        ctx.enter_context(tc.manual_schedule())
 
-        edge_rows, feat_by_pair, feat_rows = [], [], []
+        masked, feat_by_pair, feat_rows = {}, {}, {}
         w0_rows = consts.tile([P, X_PASSES * FEATURES], BF16)
         for t in range(GRAPHS):
-            edges = inputs.tile([P, CHANNELS * NODE_TILES, NODES], BF16, name="edges")
-            nc.sync.dma_start(out=edges[:], in_=edge_feat[t].rearrange("e (i p) m -> p (e i) m", p=P))
-            edge_rows.append(edges[:].rearrange("p (e i) m -> p e i m", e=CHANNELS))
-            by_pair = inputs.tile([P, PACK, FEATURES], BF16, name="by_pair")
-            nc.sync.dma_start(
-                out=by_pair[:].rearrange("p (u e) d -> p u (e d)", u=2),
-                in_=node_feat[t].rearrange("(u p e) d -> p u (e d)", u=2, e=2),
-            )
-            feat_by_pair.append(by_pair)
-            rows = inputs.tile([P, NODE_TILES, FEATURES], BF16, name="rows")
+            for e in range(CHANNELS):
+                edges = edge_pool.tile([P, NODE_TILES, NODES], BF16)
+                nc.sync.dma_start(out=edges[:], in_=edge_feat[t, e].rearrange("(i p) m -> p i m", p=P))
+                masked[CHANNELS * t + e] = edges
+                if e == 0:
+                    by_pair = feat_pool.tile([P, PACK, FEATURES], BF16)
+                    nc.sync.dma_start(
+                        out=by_pair[:].rearrange("p (u e) d -> p u (e d)", u=2),
+                        in_=node_feat[t].rearrange("(u p e) d -> p u (e d)", u=2, e=2),
+                    )
+                    feat_by_pair[t] = by_pair
+            rows = feat_pool.tile([P, NODE_TILES, FEATURES], BF16)
             nc.sync.dma_start(out=rows[:], in_=node_feat[t].rearrange("(i p) d -> p i d", p=P))
-            feat_rows.append(rows)
+            feat_rows[t] = rows
             if t == 0:
                 nc.sync.dma_start(out=w0_rows[:], in_=w0)
 
@@ -64,121 +74,241 @@ def tile_nodeupdatenetwork_pa_kernel(tc, node_feat, edge_feat, w0, out):
         def quantise(grouped, codes, scales):
             nc.vector.quantize_mx(out=codes.bitcast(FP8X4), scales=scales, in_=grouped)
 
-        def to_pair_order(matrix_rows, grouped, copy):
+        def transpose_words(matrix_rows, half):
+            bank = word_psum.tile([P, 2, HALVES * P], F32, name="bank")
+            for i in range(2):
+                row_words = matrix_rows[:, 2 * half + i, :].bitcast(F32)
+                for u in range(2):
+                    nc.tensor.transpose(bank[:, u, i * P : (i + 1) * P], row_words[:, u * P : (u + 1) * P], ident_f32[:])
+            return bank
+
+        def interleave_words(bank, grouped, half, copy):
             words = grouped.bitcast(F32).rearrange("p (r u) -> p r u", u=2)
-            for half in range(2):
-                bank = word_psum.tile([P, 2, 2 * P], F32, name="bank")
-                for i in range(2):
-                    row_words = matrix_rows[:, 2 * half + i, :].bitcast(F32)
-                    for u in range(2):
-                        nc.tensor.transpose(
-                            bank[:, u, i * P : (i + 1) * P], row_words[:, u * P : (u + 1) * P], ident_f32[:]
-                        )
-                copy(out=words[:, half * 2 * P : (half + 1) * 2 * P, :], in_=bank[:].rearrange("p u r -> p r u"))
+            copy(out=words[:, half * 2 * P : (half + 1) * 2 * P, :], in_=bank[:].rearrange("p u r -> p r u"))
 
         w0_grouped = consts.tile([P, X_PASSES, PACK * OUT_WIDTH], BF16, align_bytes=64)
         w0_codes = consts.tile([P, X_PASSES, OUT_WIDTH], U32, align_bytes=64)
         w0_scales = consts.tile([P, X_PASSES, OUT_WIDTH], U8, align_bytes=64)
-        w0_words = word_psum.tile([P, 2, P], F32, name="bank")
-        for u in range(2):
-            nc.tensor.transpose(w0_words[:, u, :], w0_rows[:].bitcast(F32)[:, u * P : (u + 1) * P], ident_f32[:])
-        nc.vector.tensor_copy(
-            out=w0_grouped[:, 0, :].bitcast(F32).rearrange("p (h u) -> p h u", u=2),
-            in_=w0_words[:].rearrange("p u h -> p h u"),
-        )
-        for g in range(1, X_PASSES):
-            w0_tiles = word_psum.tile([P, FEATURE_TILES, P], BF16, name="bank")
-            for j in range(FEATURE_TILES):
-                first = g * FEATURES + j * P
-                nc.tensor.transpose(w0_tiles[:, j, :], w0_rows[:, first : first + P], ident_bf16[:])
-            nc.vector.tensor_copy(
-                out=w0_grouped[:, g, :].rearrange("p (h j) -> p h j", j=PACK),
-                in_=w0_tiles[:].rearrange("p j h -> p h j"),
-            )
-        for g in range(X_PASSES):
-            quantise(w0_grouped[:, g, :], w0_codes[:, g, :], w0_scales[:, g, :])
+        w0_banks = {}
 
-        for t in range(GRAPHS):
-            feat_grouped = work.tile([P, PACK * FEATURES], BF16, align_bytes=64)
+        def transpose_w0():
+            w0_banks[0] = aggr_psum.tile([P, 2, P], F32, name="aggr_bank")
+            for u in range(2):
+                nc.tensor.transpose(w0_banks[0][:, u, :], w0_rows[:].bitcast(F32)[:, u * P : (u + 1) * P], ident_f32[:])
+            for g in range(1, X_PASSES):
+                w0_banks[g] = aggr_psum.tile([P, FEATURE_TILES, P], BF16, name="aggr_bank")
+                for j in range(FEATURE_TILES):
+                    first = g * FEATURES + j * P
+                    nc.tensor.transpose(w0_banks[g][:, j, :], w0_rows[:, first : first + P], ident_bf16[:])
+
+        def quantise_w0():
             nc.vector.tensor_copy(
-                out=feat_grouped[:].rearrange("p (c i v) -> p c v i", i=4, v=PACK),
+                out=w0_grouped[:, 0, :].bitcast(F32).rearrange("p (h u) -> p h u", u=2),
+                in_=w0_banks[0][:].rearrange("p u h -> p h u"),
+            )
+            for g in range(1, X_PASSES):
+                nc.vector.tensor_copy(
+                    out=w0_grouped[:, g, :].rearrange("p (h j) -> p h j", j=PACK),
+                    in_=w0_banks[g][:].rearrange("p j h -> p h j"),
+                )
+            for g in range(X_PASSES):
+                quantise(w0_grouped[:, g, :], w0_codes[:, g, :], w0_scales[:, g, :])
+
+        feat_grouped, feat_codes, feat_scales = {}, {}, {}
+        feat_banks, x0_grouped, x_codes, x_scales = {}, {}, {}, {}
+        out_banks, sloped = {}, {}
+
+        def regroup_features(t):
+            if t not in feat_by_pair:
+                return
+            feat_grouped[t] = work.tile([P, PACK * FEATURES], BF16, align_bytes=64, name="feat_grouped")
+            nc.vector.tensor_copy(
+                out=feat_grouped[t][:].rearrange("p (c i v) -> p c v i", i=4, v=PACK),
                 in_=feat_by_pair[t][:].rearrange("p v (c i) -> p c v i", i=4),
             )
-            feat_codes = work.tile([P, FEATURES], U32, align_bytes=64)
-            feat_scales = work.tile([P, FEATURES], U8, align_bytes=64)
-            quantise(feat_grouped[:], feat_codes[:], feat_scales[:])
 
-            x_codes = work.tile([P, X_PASSES, NODES], U32, align_bytes=64)
-            x_scales = work.tile([P, X_PASSES, NODES], U8, align_bytes=64)
-            x0_grouped = work.tile([P, PACK * NODES], BF16, align_bytes=64)
-            to_pair_order(feat_rows[t], x0_grouped[:], nc.scalar.copy)
-            quantise(x0_grouped[:], x_codes[:, 0, :], x_scales[:, 0, :])
+        def quantise_features(t):
+            if t not in feat_grouped:
+                return
+            feat_codes[t] = work.tile([P, FEATURES], U32, align_bytes=64, name="feat_codes")
+            feat_scales[t] = work.tile([P, FEATURES], U8, align_bytes=64, name="feat_scales")
+            quantise(feat_grouped[t][:], feat_codes[t][:], feat_scales[t][:])
 
-            masked = edge_rows[t]
-            for i in range(NODE_TILES):
-                block = masked[:, :, i, i * P : (i + 1) * P]
-                nc.vector.tensor_tensor(
-                    out=block, in0=block, in1=off_diagonal[:].unsqueeze(1).to_broadcast([P, CHANNELS, P]), op=ALU.mult
-                )
+        def transpose_features(t, half):
+            if t in feat_rows:
+                feat_banks[t, half] = transpose_words(feat_rows[t], half)
 
-            for e in range(CHANNELS):
-                denom = work.tile([P, NODE_TILES], F32)
-                for i in range(NODE_TILES):
-                    absolute = scratch.tile([P, NODES], BF16)
-                    nc.scalar.activation(
-                        out=absolute[:], in_=masked[:, e, i, :], func=ACT.Abs, accum_out=denom[:, i : i + 1]
-                    )
-                inverse = work.tile([P, NODE_TILES], F32)
-                nc.vector.tensor_scalar_max(out=inverse[:], in0=denom[:], scalar1=EPS)
-                nc.vector.reciprocal(out=inverse[:], in_=inverse[:])
-                norm_edge = work.tile([P, NODE_TILES, NODES], BF16)
-                for i in range(NODE_TILES):
-                    nc.vector.tensor_scalar(
-                        out=norm_edge[:, i, :], in0=masked[:, e, i, :], scalar1=inverse[:, i : i + 1], scalar2=None,
-                        op0=ALU.mult,
-                    )
+        def interleave_features(t, half):
+            if (t, half) not in feat_banks:
+                return
+            if half == 0:
+                x0_grouped[t] = work.tile([P, PACK * NODES], BF16, align_bytes=64, name="x0_grouped")
+            interleave_words(feat_banks[t, half], x0_grouped[t][:], half, nc.scalar.copy)
 
-                edge_grouped = work.tile([P, PACK * NODES], BF16, align_bytes=64)
-                to_pair_order(norm_edge, edge_grouped[:], nc.vector.tensor_copy)
-                edge_codes = work.tile([P, NODES], U32, align_bytes=64)
-                edge_scales = work.tile([P, NODES], U8, align_bytes=64)
-                quantise(edge_grouped[:], edge_codes[:], edge_scales[:])
+        def quantise_x0(t):
+            if t not in x0_grouped:
+                return
+            x_codes[t] = work.tile([P, X_PASSES, NODES], U32, align_bytes=64, name="x_codes")
+            x_scales[t] = work.tile([P, X_PASSES, NODES], U8, align_bytes=64, name="x_scales")
+            quantise(x0_grouped[t][:], x_codes[t][:, 0, :], x_scales[t][:, 0, :])
 
-                aggr_grouped = work.tile([P, NODES, PACK], BF16, align_bytes=64)
-                for i in range(NODE_TILES):
-                    nodes = slice(i * P, (i + 1) * P)
-                    aggr_bank = aggr_psum.tile([P, FEATURE_TILES, P], F32)
-                    for j in range(FEATURE_TILES):
-                        features = slice(j * P, (j + 1) * P)
-                        nc.tensor.matmul_mx(
-                            out=aggr_bank[:, j, :],
-                            lhsT=feat_codes[:, features].bitcast(FP8X4),
-                            lhsT_scale=feat_scales[:, features],
-                            rhs=edge_codes[:, nodes].bitcast(FP8X4),
-                            rhs_scale=edge_scales[:, nodes],
-                            start=True,
-                            stop=True,
-                        )
-                    nc.scalar.copy(out=aggr_grouped[:, nodes, :], in_=aggr_bank[:].rearrange("p j n -> p n j"))
-                quantise(
-                    aggr_grouped[:].rearrange("p n j -> p (n j)"), x_codes[:, 1 + e, :], x_scales[:, 1 + e, :]
-                )
-
-            out_bank = out_psum.tile([P, NODE_TILES, OUT_WIDTH], F32)
+        def second_matmul(t):
+            if t not in x_codes:
+                return
+            out_banks[t] = out_psum.tile([P, NODE_TILES, OUT_WIDTH], F32, name="out_bank")
             for i in range(NODE_TILES):
                 nodes = slice(i * P, (i + 1) * P)
                 for g in range(X_PASSES):
                     nc.tensor.matmul_mx(
-                        out=out_bank[:, i, :],
-                        lhsT=x_codes[:, g, nodes].bitcast(FP8X4),
-                        lhsT_scale=x_scales[:, g, nodes],
+                        out=out_banks[t][:, i, :],
+                        lhsT=x_codes[t][:, g, nodes].bitcast(FP8X4),
+                        lhsT_scale=x_scales[t][:, g, nodes],
                         rhs=w0_codes[:, g, :].bitcast(FP8X4),
                         rhs_scale=w0_scales[:, g, :],
                         start=(g == 0),
                         stop=(g == X_PASSES - 1),
                     )
-            sloped = work.tile([P, NODE_TILES, OUT_WIDTH], F32)
-            nc.scalar.activation(out=sloped[:], in_=out_bank[:], func=ACT.Copy, scale=SLOPE)
+
+        def slope(t):
+            if t not in out_banks:
+                return
+            sloped[t] = work.tile([P, NODE_TILES, OUT_WIDTH], F32, name="sloped")
+            nc.scalar.activation(out=sloped[t][:], in_=out_banks[t][:], func=ACT.Copy, scale=SLOPE)
+
+        def leaky_relu_and_store(t):
+            if t not in sloped:
+                return
             result = work.tile([P, NODE_TILES, OUT_WIDTH], F32)
-            nc.vector.tensor_tensor(out=result[:], in0=out_bank[:], in1=sloped[:], op=ALU.max)
+            nc.vector.tensor_tensor(out=result[:], in0=out_banks[t][:], in1=sloped[t][:], op=ALU.max)
             nc.sync.dma_start(out=out[t].rearrange("(i p) h -> p i h", p=P), in_=result[:])
+
+        denom, inverse, norm_edge, edge_banks, edge_grouped = {}, {}, {}, {}, {}
+        edge_codes, edge_scales, aggr_banks, aggr_grouped = {}, {}, {}, {}
+
+        def mask(s):
+            if s not in masked:
+                return
+            blocks = masked[s][:].rearrange("p i (b c) -> p (i b) c", c=P)
+            diagonal_blocks = blocks[:, 0 : NODE_TILES * NODE_TILES : NODE_TILES + 1, :]
+            nc.vector.tensor_tensor(
+                out=diagonal_blocks,
+                in0=diagonal_blocks,
+                in1=off_diagonal[:].unsqueeze(1).to_broadcast([P, NODE_TILES, P]),
+                op=ALU.mult,
+            )
+
+        def row_sums(s):
+            if s not in masked:
+                return
+            denom[s] = work.tile([P, NODE_TILES], F32, name="denom")
+            for i in range(NODE_TILES):
+                absolute = scratch.tile([P, NODES], BF16)
+                nc.scalar.activation(
+                    out=absolute[:], in_=masked[s][:, i, :], func=ACT.Abs, accum_out=denom[s][:, i : i + 1]
+                )
+
+        def clamp(s):
+            if s in denom:
+                inverse[s] = work.tile([P, NODE_TILES], F32, name="inverse")
+                nc.vector.tensor_scalar_max(out=inverse[s][:], in0=denom[s][:], scalar1=EPS)
+
+        def invert(s):
+            if s in inverse:
+                nc.vector.reciprocal(out=inverse[s][:], in_=inverse[s][:])
+
+        def normalise(s):
+            if s not in inverse:
+                return
+            norm_edge[s] = work.tile([P, NODE_TILES, NODES], BF16, name="norm_edge")
+            for i in range(NODE_TILES):
+                nc.vector.tensor_scalar(
+                    out=norm_edge[s][:, i, :], in0=masked[s][:, i, :], scalar1=inverse[s][:, i : i + 1], scalar2=None,
+                    op0=ALU.mult,
+                )
+
+        def transpose_edges(s):
+            if s in norm_edge:
+                edge_banks[s] = [transpose_words(norm_edge[s], half) for half in range(HALVES)]
+
+        def interleave_edges(s, half):
+            if s not in edge_banks:
+                return
+            if half == 0:
+                edge_grouped[s] = work.tile([P, PACK * NODES], BF16, align_bytes=64, name="edge_grouped")
+            interleave_words(edge_banks[s][half], edge_grouped[s][:], half, nc.vector.tensor_copy)
+
+        def quantise_edges(s):
+            if s not in edge_grouped:
+                return
+            edge_codes[s] = work.tile([P, NODES], U32, align_bytes=64, name="edge_codes")
+            edge_scales[s] = work.tile([P, NODES], U8, align_bytes=64, name="edge_scales")
+            quantise(edge_grouped[s][:], edge_codes[s][:], edge_scales[s][:])
+
+        def first_matmul(s):
+            if s not in edge_codes:
+                return
+            t = s // CHANNELS
+            aggr_banks[s] = []
+            for i in range(NODE_TILES):
+                nodes = slice(i * P, (i + 1) * P)
+                aggr_bank = aggr_psum.tile([P, FEATURE_TILES, P], F32)
+                for j in range(FEATURE_TILES):
+                    features = slice(j * P, (j + 1) * P)
+                    nc.tensor.matmul_mx(
+                        out=aggr_bank[:, j, :],
+                        lhsT=feat_codes[t][:, features].bitcast(FP8X4),
+                        lhsT_scale=feat_scales[t][:, features],
+                        rhs=edge_codes[s][:, nodes].bitcast(FP8X4),
+                        rhs_scale=edge_scales[s][:, nodes],
+                        start=True,
+                        stop=True,
+                    )
+                aggr_banks[s].append(aggr_bank)
+
+        def round_aggr(s):
+            if s not in aggr_banks:
+                return
+            aggr_grouped[s] = work.tile([P, NODES, PACK], BF16, align_bytes=64, name="aggr_grouped")
+            for i in range(NODE_TILES):
+                nc.scalar.copy(
+                    out=aggr_grouped[s][:, i * P : (i + 1) * P, :], in_=aggr_banks[s][i][:].rearrange("p j n -> p n j")
+                )
+
+        def quantise_aggr(s):
+            if s not in aggr_grouped:
+                return
+            t, e = divmod(s, CHANNELS)
+            quantise(
+                aggr_grouped[s][:].rearrange("p n j -> p (n j)"), x_codes[t][:, 1 + e, :], x_scales[t][:, 1 + e, :]
+            )
+
+        for step in range(-3, UNITS + 2):
+            graph, second_step = divmod(step, CHANNELS)
+            mask(step + 3)
+            row_sums(step + 2)
+            interleave_features(*divmod(step + 1, HALVES))
+            if second_step:
+                quantise_features(graph + 1)
+                quantise_x0(graph)
+                leaky_relu_and_store(graph - 1)
+            else:
+                regroup_features(graph + 1)
+            interleave_edges(step + 1, 0)
+            clamp(step + 2)
+            interleave_edges(step + 1, 1)
+            invert(step + 2)
+            quantise_aggr(step - 1)
+            if not second_step:
+                second_matmul(graph - 1)
+            normalise(step + 2)
+            transpose_edges(step + 2)
+            transpose_features(*divmod(step + 2, HALVES))
+            quantise_edges(step + 1)
+            if step == W0_STEP:
+                quantise_w0()
+            round_aggr(step)
+            if not second_step:
+                slope(graph - 1)
+            first_matmul(step + 1)
+            if step == W0_STEP - 1:
+                transpose_w0()

@@ -235,7 +235,8 @@ def tile_nodeupdatenetwork_pa_kernel(tc, node_feat, edge_feat, w0, out):
                 return
             if half == 0:
                 edge_grouped[s] = work.tile([P, PACK * NODES], BF16, align_bytes=64, name="edge_grouped")
-            interleave_words(edge_banks[s][half], edge_grouped[s][:], half, nc.vector.tensor_copy)
+            copy = nc.scalar.copy if half == 0 else nc.vector.tensor_copy
+            interleave_words(edge_banks[s][half], edge_grouped[s][:], half, copy)
 
         def quantise_edges(s):
             if s not in edge_grouped:
@@ -265,27 +266,36 @@ def tile_nodeupdatenetwork_pa_kernel(tc, node_feat, edge_feat, w0, out):
                     )
                 aggr_banks[s].append(aggr_bank)
 
-        def round_aggr(s):
+        def round_aggr(s, on_vector):
             if s not in aggr_banks:
                 return
-            aggr_grouped[s] = work.tile([P, NODES, PACK], BF16, align_bytes=64, name="aggr_grouped")
+            if s not in aggr_grouped:
+                aggr_grouped[s] = work.tile([P, NODES, PACK], BF16, align_bytes=64, name="aggr_grouped")
+            copy = nc.vector.tensor_copy if on_vector else nc.scalar.copy
             for i in range(NODE_TILES):
-                nc.scalar.copy(
-                    out=aggr_grouped[s][:, i * P : (i + 1) * P, :], in_=aggr_banks[s][i][:].rearrange("p j n -> p n j")
-                )
+                if ((NODE_TILES * s + i) % 3 == 2) == on_vector:
+                    copy(
+                        out=aggr_grouped[s][:, i * P : (i + 1) * P, :],
+                        in_=aggr_banks[s][i][:].rearrange("p j n -> p n j"),
+                    )
 
         def quantise_aggr(s):
             if s not in aggr_grouped:
                 return
             t, e = divmod(s, CHANNELS)
-            quantise(
-                aggr_grouped[s][:].rearrange("p n j -> p (n j)"), x_codes[t][:, 1 + e, :], x_scales[t][:, 1 + e, :]
-            )
+            for i in range(NODE_TILES):
+                nodes = slice(i * P, (i + 1) * P)
+                quantise(
+                    aggr_grouped[s][:, nodes, :].rearrange("p n j -> p (n j)"),
+                    x_codes[t][:, 1 + e, nodes],
+                    x_scales[t][:, 1 + e, nodes],
+                )
 
         for step in range(-3, UNITS + 2):
             graph, second_step = divmod(step, CHANNELS)
             mask(step + 3)
             row_sums(step + 2)
+            interleave_edges(step + 1, 0)
             interleave_features(*divmod(step + 1, HALVES))
             if second_step:
                 quantise_features(graph + 1)
@@ -293,20 +303,20 @@ def tile_nodeupdatenetwork_pa_kernel(tc, node_feat, edge_feat, w0, out):
                 leaky_relu_and_store(graph - 1)
             else:
                 regroup_features(graph + 1)
-            interleave_edges(step + 1, 0)
-            clamp(step + 2)
-            interleave_edges(step + 1, 1)
-            invert(step + 2)
             quantise_aggr(step - 1)
             if not second_step:
                 second_matmul(graph - 1)
+            clamp(step + 2)
+            interleave_edges(step + 1, 1)
+            invert(step + 2)
+            round_aggr(step, True)
             normalise(step + 2)
             transpose_edges(step + 2)
             transpose_features(*divmod(step + 2, HALVES))
             quantise_edges(step + 1)
             if step == W0_STEP:
                 quantise_w0()
-            round_aggr(step)
+            round_aggr(step, False)
             if not second_step:
                 slope(graph - 1)
             first_matmul(step + 1)

@@ -6,6 +6,7 @@ from concourse.masks import make_identity
 F32 = mybir.dt.float32
 BF16 = mybir.dt.bfloat16
 U32 = mybir.dt.uint32
+I32 = mybir.dt.int32
 U8 = mybir.dt.uint8
 FP8X4 = mybir.dt.float8_e4m3fn_x4
 ALU = mybir.AluOpType
@@ -19,6 +20,7 @@ FEATURE_TILES = FEATURES // P
 X_PASSES = 1 + CHANNELS
 EPS = 1e-12
 SLOPE = 0.01
+SIGN_CLEARED = 0x7FFF7FFF
 
 W0_STEP = -1
 
@@ -36,31 +38,48 @@ def tile_nodeupdatenetwork_pa_kernel(tc, node_feat, edge_feat, w0, out):
         edge_pool = ctx.enter_context(tc.tile_pool(name="edge_pool", bufs=UNITS))
         feat_pool = ctx.enter_context(tc.tile_pool(name="feat_pool", bufs=GRAPHS))
         work = ctx.enter_context(tc.tile_pool(name="work", bufs=2))
+        small = ctx.enter_context(tc.tile_pool(name="small", bufs=4))
         scratch = ctx.enter_context(tc.tile_pool(name="scratch", bufs=4))
         word_psum = ctx.enter_context(tc.psum_pool(name="word_psum", bufs=3))
         aggr_psum = ctx.enter_context(tc.psum_pool(name="aggr_psum", bufs=NODE_TILES))
         out_psum = ctx.enter_context(tc.psum_pool(name="out_psum", bufs=1))
         ctx.enter_context(tc.manual_schedule())
 
+        table_seed = consts.tile([P, 1], F32)
+        table_ready = consts.tile([P, 1], F32)
+        nc.vector.memset(table_seed[:], 0.0)
+        nc.scalar.activation(out=table_ready[:], in_=table_seed[:], func=ACT.Abs)
+
         masked, feat_by_pair, feat_rows = {}, {}, {}
         w0_rows = consts.tile([P, X_PASSES * FEATURES], BF16)
+
+        def load_edges(s):
+            if s >= UNITS:
+                return
+            t, e = divmod(s, CHANNELS)
+            masked[s] = edge_pool.tile([P, NODE_TILES, NODES], BF16, name="edges")
+            tiles_in_a_load = 1 if s == 0 else NODE_TILES
+            for i in range(0, NODE_TILES, tiles_in_a_load):
+                nc.sync.dma_start(
+                    out=masked[s][:, i : i + tiles_in_a_load, :],
+                    in_=edge_feat[t, e, i * P : (i + tiles_in_a_load) * P, :].rearrange("(i p) m -> p i m", p=P),
+                )
+
+        load_edges(0)
+        load_edges(2)
         for t in range(GRAPHS):
-            for e in range(CHANNELS):
-                edges = edge_pool.tile([P, NODE_TILES, NODES], BF16)
-                nc.sync.dma_start(out=edges[:], in_=edge_feat[t, e].rearrange("(i p) m -> p i m", p=P))
-                masked[CHANNELS * t + e] = edges
-                if e == 0:
-                    by_pair = feat_pool.tile([P, PACK, FEATURES], BF16)
-                    nc.sync.dma_start(
-                        out=by_pair[:].rearrange("p (u e) d -> p u (e d)", u=2),
-                        in_=node_feat[t].rearrange("(u p e) d -> p u (e d)", u=2, e=2),
-                    )
-                    feat_by_pair[t] = by_pair
-            rows = feat_pool.tile([P, NODE_TILES, FEATURES], BF16)
-            nc.sync.dma_start(out=rows[:], in_=node_feat[t].rearrange("(i p) d -> p i d", p=P))
-            feat_rows[t] = rows
+            feat_by_pair[t] = feat_pool.tile([P, PACK, FEATURES], BF16, name="by_pair")
+            nc.sync.dma_start(
+                out=feat_by_pair[t][:].rearrange("p (u e) d -> p u (e d)", u=2),
+                in_=node_feat[t].rearrange("(u p e) d -> p u (e d)", u=2, e=2),
+            )
+            load_edges(CHANNELS * t + 1)
+            if t > 0:
+                load_edges(CHANNELS * t + 2)
             if t == 0:
                 nc.sync.dma_start(out=w0_rows[:], in_=w0)
+            feat_rows[t] = feat_pool.tile([P, NODE_TILES, FEATURES], BF16, name="rows")
+            nc.sync.dma_start(out=feat_rows[t][:], in_=node_feat[t].rearrange("(i p) d -> p i d", p=P))
 
         ident_f32 = consts.tile([P, P], F32)
         make_identity(nc, ident_f32[:])
@@ -92,25 +111,27 @@ def tile_nodeupdatenetwork_pa_kernel(tc, node_feat, edge_feat, w0, out):
         w0_banks = {}
 
         def transpose_w0():
-            w0_banks[0] = aggr_psum.tile([P, 2, P], F32, name="aggr_bank")
+            w0_banks[0] = word_psum.tile([P, 2, P], F32, name="bank")
             for u in range(2):
                 nc.tensor.transpose(w0_banks[0][:, u, :], w0_rows[:].bitcast(F32)[:, u * P : (u + 1) * P], ident_f32[:])
             for g in range(1, X_PASSES):
-                w0_banks[g] = aggr_psum.tile([P, FEATURE_TILES, P], BF16, name="aggr_bank")
+                w0_banks[g] = word_psum.tile([P, FEATURE_TILES, P], BF16, name="bank")
                 for j in range(FEATURE_TILES):
                     first = g * FEATURES + j * P
                     nc.tensor.transpose(w0_banks[g][:, j, :], w0_rows[:, first : first + P], ident_bf16[:])
 
-        def quantise_w0():
-            nc.vector.tensor_copy(
+        def interleave_w0():
+            nc.scalar.copy(
                 out=w0_grouped[:, 0, :].bitcast(F32).rearrange("p (h u) -> p h u", u=2),
                 in_=w0_banks[0][:].rearrange("p u h -> p h u"),
             )
             for g in range(1, X_PASSES):
-                nc.vector.tensor_copy(
+                nc.scalar.copy(
                     out=w0_grouped[:, g, :].rearrange("p (h j) -> p h j", j=PACK),
                     in_=w0_banks[g][:].rearrange("p j h -> p h j"),
                 )
+
+        def quantise_w0():
             for g in range(X_PASSES):
                 quantise(w0_grouped[:, g, :], w0_codes[:, g, :], w0_scales[:, g, :])
 
@@ -155,12 +176,17 @@ def tile_nodeupdatenetwork_pa_kernel(tc, node_feat, edge_feat, w0, out):
         def second_matmul(t):
             if t not in x_codes:
                 return
-            out_banks[t] = out_psum.tile([P, NODE_TILES, OUT_WIDTH], F32, name="out_bank")
+            tiles_in_a_bank = NODE_TILES // 2 if t == GRAPHS - 1 else NODE_TILES
+            out_banks[t] = []
             for i in range(NODE_TILES):
                 nodes = slice(i * P, (i + 1) * P)
+                if i == 0:
+                    out_banks[t].append(out_psum.tile([P, tiles_in_a_bank, OUT_WIDTH], F32, name="out_bank"))
+                elif i == tiles_in_a_bank:
+                    out_banks[t].append(word_psum.tile([P, tiles_in_a_bank, OUT_WIDTH], F32, name="bank"))
                 for g in range(X_PASSES):
                     nc.tensor.matmul_mx(
-                        out=out_banks[t][:, i, :],
+                        out=out_banks[t][-1][:, i % tiles_in_a_bank, :],
                         lhsT=x_codes[t][:, g, nodes].bitcast(FP8X4),
                         lhsT_scale=x_scales[t][:, g, nodes],
                         rhs=w0_codes[:, g, :].bitcast(FP8X4),
@@ -172,21 +198,36 @@ def tile_nodeupdatenetwork_pa_kernel(tc, node_feat, edge_feat, w0, out):
         def slope(t):
             if t not in out_banks:
                 return
-            sloped[t] = work.tile([P, NODE_TILES, OUT_WIDTH], F32, name="sloped")
-            nc.scalar.activation(out=sloped[t][:], in_=out_banks[t][:], func=ACT.Copy, scale=SLOPE)
+            sloped[t] = []
+            for bank in out_banks[t]:
+                times_slope = work.tile(bank.shape, F32, name="times_slope")
+                nc.scalar.activation(out=times_slope[:], in_=bank[:], func=ACT.Copy, scale=SLOPE)
+                sloped[t].append(times_slope)
 
         def leaky_relu_and_store(t):
             if t not in sloped:
                 return
-            result = work.tile([P, NODE_TILES, OUT_WIDTH], F32)
-            nc.vector.tensor_tensor(out=result[:], in0=out_banks[t][:], in1=sloped[t][:], op=ALU.max)
-            nc.sync.dma_start(out=out[t].rearrange("(i p) h -> p i h", p=P), in_=result[:])
+            first_row = 0
+            for bank, times_slope in zip(out_banks[t], sloped[t]):
+                result = work.tile(bank.shape, F32, name="result")
+                nc.vector.tensor_tensor(out=result[:], in0=bank[:], in1=times_slope[:], op=ALU.max)
+                end_row = first_row + bank.shape[1] * P
+                nc.sync.dma_start(
+                    out=out[t, first_row:end_row, :].rearrange("(i p) h -> p i h", p=P), in_=result[:]
+                )
+                first_row = end_row
 
         denom, inverse, norm_edge, edge_banks, edge_grouped = {}, {}, {}, {}, {}
         edge_codes, edge_scales, aggr_banks, aggr_grouped = {}, {}, {}, {}
+        magnitudes, folded = {}, {}
 
         def mask(s):
             if s not in masked:
+                return
+            if s == 0:
+                for i in range(NODE_TILES):
+                    diagonal_block = masked[s][:, i, i * P : (i + 1) * P]
+                    nc.vector.tensor_tensor(out=diagonal_block, in0=diagonal_block, in1=off_diagonal[:], op=ALU.mult)
                 return
             blocks = masked[s][:].rearrange("p i (b c) -> p (i b) c", c=P)
             diagonal_blocks = blocks[:, 0 : NODE_TILES * NODE_TILES : NODE_TILES + 1, :]
@@ -197,19 +238,52 @@ def tile_nodeupdatenetwork_pa_kernel(tc, node_feat, edge_feat, w0, out):
                 op=ALU.mult,
             )
 
-        def row_sums(s):
-            if s not in masked:
+        def scalar_row_sums(s, half):
+            if s not in masked or s % CHANNELS == 1:
                 return
-            denom[s] = work.tile([P, NODE_TILES], F32, name="denom")
-            for i in range(NODE_TILES):
+            if half == 0:
+                denom[s] = small.tile([P, NODE_TILES], F32, name="denom")
+            for i in range(2 * half, 2 * half + 2):
                 absolute = scratch.tile([P, NODES], BF16)
                 nc.scalar.activation(
                     out=absolute[:], in_=masked[s][:, i, :], func=ACT.Abs, accum_out=denom[s][:, i : i + 1]
                 )
 
+        def clear_signs(s):
+            if s not in masked or s % CHANNELS == 0:
+                return
+            magnitudes[s] = work.tile([P, NODE_TILES, NODES], BF16, name="magnitudes")
+            nc.vector.tensor_scalar(
+                out=magnitudes[s][:].rearrange("p i m -> p (i m)").bitcast(I32),
+                in0=masked[s][:].rearrange("p i m -> p (i m)").bitcast(I32),
+                scalar1=SIGN_CLEARED, scalar2=None, op0=ALU.bitwise_and,
+            )
+
+        def fold_columns(s):
+            if s not in magnitudes:
+                return
+            folded[s] = out_psum.tile([P, NODE_TILES, P], F32, name="out_bank")
+            for b in range(NODES // P):
+                nc.tensor.matmul(
+                    out=folded[s][:], lhsT=ident_bf16[:], rhs=magnitudes[s][:, :, b * P : (b + 1) * P],
+                    start=(b == 0), stop=(b == NODES // P - 1),
+                )
+
+        def vector_row_sums(s):
+            if s == 0:
+                nc.vector.tensor_reduce(
+                    out=denom[s][:, 2:4], in_=masked[s][:, 2:4, :], axis=mybir.AxisListType.X, op=ALU.add,
+                    apply_absolute_value=True,
+                )
+                return
+            if s not in folded:
+                return
+            denom[s] = small.tile([P, NODE_TILES], F32, name="denom")
+            nc.vector.tensor_reduce(out=denom[s][:], in_=folded[s][:], axis=mybir.AxisListType.X, op=ALU.add)
+
         def clamp(s):
             if s in denom:
-                inverse[s] = work.tile([P, NODE_TILES], F32, name="inverse")
+                inverse[s] = small.tile([P, NODE_TILES], F32, name="inverse")
                 nc.vector.tensor_scalar_max(out=inverse[s][:], in0=denom[s][:], scalar1=EPS)
 
         def invert(s):
@@ -235,7 +309,7 @@ def tile_nodeupdatenetwork_pa_kernel(tc, node_feat, edge_feat, w0, out):
                 return
             if half == 0:
                 edge_grouped[s] = work.tile([P, PACK * NODES], BF16, align_bytes=64, name="edge_grouped")
-            copy = nc.scalar.copy if half == 0 else nc.vector.tensor_copy
+            copy = nc.vector.tensor_copy if half == 1 and s % CHANNELS == 1 else nc.scalar.copy
             interleave_words(edge_banks[s][half], edge_grouped[s][:], half, copy)
 
         def quantise_edges(s):
@@ -273,7 +347,8 @@ def tile_nodeupdatenetwork_pa_kernel(tc, node_feat, edge_feat, w0, out):
                 aggr_grouped[s] = work.tile([P, NODES, PACK], BF16, align_bytes=64, name="aggr_grouped")
             copy = nc.vector.tensor_copy if on_vector else nc.scalar.copy
             for i in range(NODE_TILES):
-                if ((NODE_TILES * s + i) % 3 == 2) == on_vector:
+                vectors = i % 2 == 1 if s == UNITS - 1 else s % CHANNELS == 0 and i == 0
+                if vectors == on_vector:
                     copy(
                         out=aggr_grouped[s][:, i * P : (i + 1) * P, :],
                         in_=aggr_banks[s][i][:].rearrange("p j n -> p n j"),
@@ -283,42 +358,82 @@ def tile_nodeupdatenetwork_pa_kernel(tc, node_feat, edge_feat, w0, out):
             if s not in aggr_grouped:
                 return
             t, e = divmod(s, CHANNELS)
-            for i in range(NODE_TILES):
-                nodes = slice(i * P, (i + 1) * P)
+            width = P if s == UNITS - 1 else NODES
+            for first in range(0, NODES, width):
+                nodes = slice(first, first + width)
                 quantise(
                     aggr_grouped[s][:, nodes, :].rearrange("p n j -> p (n j)"),
                     x_codes[t][:, 1 + e, nodes],
                     x_scales[t][:, 1 + e, nodes],
                 )
 
-        for step in range(-3, UNITS + 2):
+        mask(0)
+        scalar_row_sums(0, 0)
+        vector_row_sums(0)
+        mask(2)
+        scalar_row_sums(2, 0)
+        clamp(0)
+        invert(0)
+        normalise(0)
+        transpose_edges(0)
+        regroup_features(0)
+        mask(1)
+        quantise_features(0)
+        clear_signs(1)
+        interleave_edges(0, 0)
+        interleave_edges(0, 1)
+        transpose_w0()
+        fold_columns(1)
+        quantise_edges(0)
+        first_matmul(0)
+        scalar_row_sums(2, 1)
+        interleave_w0()
+        vector_row_sums(1)
+        clamp(1)
+        mask(3)
+        invert(1)
+        clear_signs(3)
+        normalise(1)
+        transpose_features(0, 0)
+        transpose_edges(1)
+        interleave_features(0, 0)
+        transpose_features(0, 1)
+        fold_columns(3)
+        quantise_w0()
+        mask(4)
+        regroup_features(1)
+        for step in range(UNITS + 2):
             graph, second_step = divmod(step, CHANNELS)
-            mask(step + 3)
-            row_sums(step + 2)
+            scalar_row_sums(step + 3, 0)
+            if step:
+                scalar_row_sums(step + 2, 1)
             interleave_edges(step + 1, 0)
             interleave_features(*divmod(step + 1, HALVES))
             if second_step:
-                quantise_features(graph + 1)
                 quantise_x0(graph)
-                leaky_relu_and_store(graph - 1)
             else:
-                regroup_features(graph + 1)
+                quantise_features(graph + 1)
+            interleave_edges(step + 1, 1)
+            vector_row_sums(step + 3)
             quantise_aggr(step - 1)
             if not second_step:
                 second_matmul(graph - 1)
             clamp(step + 2)
-            interleave_edges(step + 1, 1)
-            invert(step + 2)
             round_aggr(step, True)
+            invert(step + 2)
+            if second_step:
+                leaky_relu_and_store(graph - 1)
+                clear_signs(step + 4)
             normalise(step + 2)
             transpose_edges(step + 2)
             transpose_features(*divmod(step + 2, HALVES))
+            if second_step:
+                fold_columns(step + 4)
             quantise_edges(step + 1)
-            if step == W0_STEP:
-                quantise_w0()
+            mask(step + 5)
             round_aggr(step, False)
-            if not second_step:
+            if second_step:
+                regroup_features(graph + 2)
+            else:
                 slope(graph - 1)
             first_matmul(step + 1)
-            if step == W0_STEP - 1:
-                transpose_w0()

@@ -38,6 +38,7 @@ def tile_nodeupdatenetwork_pa_kernel(tc, node_feat, edge_feat, w0, out):
         edge_pool = ctx.enter_context(tc.tile_pool(name="edge_pool", bufs=UNITS))
         feat_pool = ctx.enter_context(tc.tile_pool(name="feat_pool", bufs=GRAPHS))
         work = ctx.enter_context(tc.tile_pool(name="work", bufs=2))
+        outputs = ctx.enter_context(tc.tile_pool(name="outputs", bufs=4))
         small = ctx.enter_context(tc.tile_pool(name="small", bufs=4))
         scratch = ctx.enter_context(tc.tile_pool(name="scratch", bufs=4))
         word_psum = ctx.enter_context(tc.psum_pool(name="word_psum", bufs=3))
@@ -74,8 +75,7 @@ def tile_nodeupdatenetwork_pa_kernel(tc, node_feat, edge_feat, w0, out):
                 in_=node_feat[t].rearrange("(u p e) d -> p u (e d)", u=2, e=2),
             )
             load_edges(CHANNELS * t + 1)
-            if t > 0:
-                load_edges(CHANNELS * t + 2)
+            load_edges(CHANNELS * t + 4)
             if t == 0:
                 nc.sync.dma_start(out=w0_rows[:], in_=w0)
             feat_rows[t] = feat_pool.tile([P, NODE_TILES, FEATURES], BF16, name="rows")
@@ -121,12 +121,12 @@ def tile_nodeupdatenetwork_pa_kernel(tc, node_feat, edge_feat, w0, out):
                     nc.tensor.transpose(w0_banks[g][:, j, :], w0_rows[:, first : first + P], ident_bf16[:])
 
         def interleave_w0():
-            nc.scalar.copy(
+            nc.vector.tensor_copy(
                 out=w0_grouped[:, 0, :].bitcast(F32).rearrange("p (h u) -> p h u", u=2),
                 in_=w0_banks[0][:].rearrange("p u h -> p h u"),
             )
             for g in range(1, X_PASSES):
-                nc.scalar.copy(
+                nc.vector.tensor_copy(
                     out=w0_grouped[:, g, :].rearrange("p (h j) -> p h j", j=PACK),
                     in_=w0_banks[g][:].rearrange("p j h -> p h j"),
                 )
@@ -180,10 +180,12 @@ def tile_nodeupdatenetwork_pa_kernel(tc, node_feat, edge_feat, w0, out):
             out_banks[t] = []
             for i in range(NODE_TILES):
                 nodes = slice(i * P, (i + 1) * P)
-                if i == 0:
-                    out_banks[t].append(out_psum.tile([P, tiles_in_a_bank, OUT_WIDTH], F32, name="out_bank"))
-                elif i == tiles_in_a_bank:
-                    out_banks[t].append(word_psum.tile([P, tiles_in_a_bank, OUT_WIDTH], F32, name="bank"))
+                if i % tiles_in_a_bank == 0:
+                    if t == GRAPHS - 1:
+                        out_bank = word_psum.tile([P, tiles_in_a_bank, OUT_WIDTH], F32, name="bank")
+                    else:
+                        out_bank = out_psum.tile([P, tiles_in_a_bank, OUT_WIDTH], F32, name="out_bank")
+                    out_banks[t].append(out_bank)
                 for g in range(X_PASSES):
                     nc.tensor.matmul_mx(
                         out=out_banks[t][-1][:, i % tiles_in_a_bank, :],
@@ -200,7 +202,7 @@ def tile_nodeupdatenetwork_pa_kernel(tc, node_feat, edge_feat, w0, out):
                 return
             sloped[t] = []
             for bank in out_banks[t]:
-                times_slope = work.tile(bank.shape, F32, name="times_slope")
+                times_slope = outputs.tile(bank.shape, F32, name="times_slope")
                 nc.scalar.activation(out=times_slope[:], in_=bank[:], func=ACT.Copy, scale=SLOPE)
                 sloped[t].append(times_slope)
 
@@ -208,8 +210,8 @@ def tile_nodeupdatenetwork_pa_kernel(tc, node_feat, edge_feat, w0, out):
             if t not in sloped:
                 return
             first_row = 0
-            for bank, times_slope in zip(out_banks[t], sloped[t]):
-                result = work.tile(bank.shape, F32, name="result")
+            for bank, times_slope in zip(out_banks[t], sloped.pop(t)):
+                result = outputs.tile(bank.shape, F32, name="result")
                 nc.vector.tensor_tensor(out=result[:], in0=bank[:], in1=times_slope[:], op=ALU.max)
                 end_row = first_row + bank.shape[1] * P
                 nc.sync.dma_start(
@@ -243,7 +245,7 @@ def tile_nodeupdatenetwork_pa_kernel(tc, node_feat, edge_feat, w0, out):
                 return
             if half == 0:
                 denom[s] = small.tile([P, NODE_TILES], F32, name="denom")
-            for i in range(2 * half, 2 * half + 2):
+            for i in range(2 * half, 3 if s == 0 and half == 1 else 2 * half + 2):
                 absolute = scratch.tile([P, NODES], BF16)
                 nc.scalar.activation(
                     out=absolute[:], in_=masked[s][:, i, :], func=ACT.Abs, accum_out=denom[s][:, i : i + 1]
@@ -272,7 +274,7 @@ def tile_nodeupdatenetwork_pa_kernel(tc, node_feat, edge_feat, w0, out):
         def vector_row_sums(s):
             if s == 0:
                 nc.vector.tensor_reduce(
-                    out=denom[s][:, 2:4], in_=masked[s][:, 2:4, :], axis=mybir.AxisListType.X, op=ALU.add,
+                    out=denom[s][:, 3:4], in_=masked[s][:, 3:4, :], axis=mybir.AxisListType.X, op=ALU.add,
                     apply_absolute_value=True,
                 )
                 return
@@ -319,12 +321,12 @@ def tile_nodeupdatenetwork_pa_kernel(tc, node_feat, edge_feat, w0, out):
             edge_scales[s] = work.tile([P, NODES], U8, align_bytes=64, name="edge_scales")
             quantise(edge_grouped[s][:], edge_codes[s][:], edge_scales[s][:])
 
-        def first_matmul(s):
+        def first_matmul(s, node_tiles):
             if s not in edge_codes:
                 return
             t = s // CHANNELS
-            aggr_banks[s] = []
-            for i in range(NODE_TILES):
+            aggr_banks.setdefault(s, [])
+            for i in node_tiles:
                 nodes = slice(i * P, (i + 1) * P)
                 aggr_bank = aggr_psum.tile([P, FEATURE_TILES, P], F32)
                 for j in range(FEATURE_TILES):
@@ -340,19 +342,18 @@ def tile_nodeupdatenetwork_pa_kernel(tc, node_feat, edge_feat, w0, out):
                     )
                 aggr_banks[s].append(aggr_bank)
 
-        def round_aggr(s, on_vector):
+        def round_aggr(s, node_tiles):
             if s not in aggr_banks:
                 return
             if s not in aggr_grouped:
                 aggr_grouped[s] = work.tile([P, NODES, PACK], BF16, align_bytes=64, name="aggr_grouped")
-            copy = nc.vector.tensor_copy if on_vector else nc.scalar.copy
-            for i in range(NODE_TILES):
-                vectors = i % 2 == 1 if s == UNITS - 1 else s % CHANNELS == 0 and i == 0
-                if vectors == on_vector:
-                    copy(
-                        out=aggr_grouped[s][:, i * P : (i + 1) * P, :],
-                        in_=aggr_banks[s][i][:].rearrange("p j n -> p n j"),
-                    )
+            for i in node_tiles:
+                vectors = i % 2 == 1 if s == UNITS - 1 else s in (4, 6) and i == 3
+                copy = nc.vector.tensor_copy if vectors else nc.scalar.copy
+                copy(
+                    out=aggr_grouped[s][:, i * P : (i + 1) * P, :],
+                    in_=aggr_banks[s][i][:].rearrange("p j n -> p n j"),
+                )
 
         def quantise_aggr(s):
             if s not in aggr_grouped:
@@ -369,6 +370,7 @@ def tile_nodeupdatenetwork_pa_kernel(tc, node_feat, edge_feat, w0, out):
 
         mask(0)
         scalar_row_sums(0, 0)
+        scalar_row_sums(0, 1)
         vector_row_sums(0)
         mask(2)
         scalar_row_sums(2, 0)
@@ -380,60 +382,63 @@ def tile_nodeupdatenetwork_pa_kernel(tc, node_feat, edge_feat, w0, out):
         mask(1)
         quantise_features(0)
         clear_signs(1)
+        mask(4)
         interleave_edges(0, 0)
         interleave_edges(0, 1)
+        scalar_row_sums(2, 1)
+        scalar_row_sums(4, 0)
         transpose_w0()
         fold_columns(1)
         quantise_edges(0)
-        first_matmul(0)
-        scalar_row_sums(2, 1)
+        first_matmul(0, range(4))
         interleave_w0()
         vector_row_sums(1)
         clamp(1)
         mask(3)
         invert(1)
+        transpose_features(0, 0)
+        interleave_features(0, 0)
+        scalar_row_sums(4, 1)
         clear_signs(3)
         normalise(1)
-        transpose_features(0, 0)
         transpose_edges(1)
-        interleave_features(0, 0)
         transpose_features(0, 1)
         fold_columns(3)
         quantise_w0()
-        mask(4)
+        clamp(2)
         regroup_features(1)
-        for step in range(UNITS + 2):
+        invert(2)
+        for step in range(UNITS + 3):
             graph, second_step = divmod(step, CHANNELS)
-            scalar_row_sums(step + 3, 0)
-            if step:
-                scalar_row_sums(step + 2, 1)
             interleave_edges(step + 1, 0)
+            interleave_edges(step + 1, 1)
+            mask(step + 5)
+            normalise(step + 2)
+            transpose_edges(step + 2)
             interleave_features(*divmod(step + 1, HALVES))
             if second_step:
                 quantise_x0(graph)
-            else:
-                quantise_features(graph + 1)
-            interleave_edges(step + 1, 1)
-            vector_row_sums(step + 3)
             quantise_aggr(step - 1)
             if not second_step:
-                second_matmul(graph - 1)
-            clamp(step + 2)
-            round_aggr(step, True)
-            invert(step + 2)
-            if second_step:
-                leaky_relu_and_store(graph - 1)
-                clear_signs(step + 4)
-            normalise(step + 2)
-            transpose_edges(step + 2)
+                vector_row_sums(step + 3)
+                leaky_relu_and_store(graph - 2)
             transpose_features(*divmod(step + 2, HALVES))
-            if second_step:
-                fold_columns(step + 4)
             quantise_edges(step + 1)
-            mask(step + 5)
-            round_aggr(step, False)
+            clamp(step + 3)
+            round_aggr(step, range(4))
+            first_matmul(step + 1, range(4))
             if second_step:
                 regroup_features(graph + 2)
-            else:
                 slope(graph - 1)
-            first_matmul(step + 1)
+                invert(step + 3)
+                clear_signs(step + 4)
+                if step + 4 < UNITS:
+                    leaky_relu_and_store(graph - 1)
+                    fold_columns(step + 4)
+            else:
+                invert(step + 3)
+                quantise_features(graph + 1)
+                second_matmul(graph - 1)
+            scalar_row_sums(step + 5, 0)
+            if step:
+                scalar_row_sums(step + 4, 1)

@@ -66,20 +66,30 @@ def tile_nodeupdatenetwork_pa_kernel(tc, node_feat, edge_feat, w0, out):
                     in_=edge_feat[t, e, i * P : (i + tiles_in_a_load) * P, :].rearrange("(i p) m -> p i m", p=P),
                 )
 
-        load_edges(0)
-        load_edges(2)
-        for t in range(GRAPHS):
+        def load_rows(t):
+            feat_rows[t] = feat_pool.tile([P, NODE_TILES, FEATURES], BF16, name="rows")
+            nc.sync.dma_start(out=feat_rows[t][:], in_=node_feat[t].rearrange("(i p) d -> p i d", p=P))
+
+        def load_features_by_pair(t):
+            if t >= GRAPHS:
+                return
             feat_by_pair[t] = feat_pool.tile([P, PACK, FEATURES], BF16, name="by_pair")
             nc.sync.dma_start(
                 out=feat_by_pair[t][:].rearrange("p (u e) d -> p u (e d)", u=2),
                 in_=node_feat[t].rearrange("(u p e) d -> p u (e d)", u=2, e=2),
             )
-            load_edges(CHANNELS * t + 1)
-            load_edges(CHANNELS * t + 4)
-            if t == 0:
+
+        order_of_need = [0, 2, 1, 4, 3, 5, 6, 7]
+        for t in range(GRAPHS):
+            for s in order_of_need[2 * t : 2 * t + 2]:
+                load_edges(s)
+            if t == 1:
                 nc.sync.dma_start(out=w0_rows[:], in_=w0)
-            feat_rows[t] = feat_pool.tile([P, NODE_TILES, FEATURES], BF16, name="rows")
-            nc.sync.dma_start(out=feat_rows[t][:], in_=node_feat[t].rearrange("(i p) d -> p i d", p=P))
+            load_features_by_pair(t)
+            if t == 0:
+                continue
+            load_rows(t - 1)
+        load_rows(GRAPHS - 1)
 
         ident_f32 = consts.tile([P, P], F32)
         make_identity(nc, ident_f32[:])
@@ -121,12 +131,12 @@ def tile_nodeupdatenetwork_pa_kernel(tc, node_feat, edge_feat, w0, out):
                     nc.tensor.transpose(w0_banks[g][:, j, :], w0_rows[:, first : first + P], ident_bf16[:])
 
         def interleave_w0():
-            nc.vector.tensor_copy(
+            nc.scalar.copy(
                 out=w0_grouped[:, 0, :].bitcast(F32).rearrange("p (h u) -> p h u", u=2),
                 in_=w0_banks[0][:].rearrange("p u h -> p h u"),
             )
             for g in range(1, X_PASSES):
-                nc.vector.tensor_copy(
+                nc.scalar.copy(
                     out=w0_grouped[:, g, :].rearrange("p (h j) -> p h j", j=PACK),
                     in_=w0_banks[g][:].rearrange("p j h -> p h j"),
                 )
@@ -388,10 +398,11 @@ def tile_nodeupdatenetwork_pa_kernel(tc, node_feat, edge_feat, w0, out):
         scalar_row_sums(2, 1)
         scalar_row_sums(4, 0)
         transpose_w0()
+        interleave_w0()
         fold_columns(1)
         quantise_edges(0)
+        regroup_features(1)
         first_matmul(0, range(4))
-        interleave_w0()
         vector_row_sums(1)
         clamp(1)
         mask(3)
@@ -406,7 +417,6 @@ def tile_nodeupdatenetwork_pa_kernel(tc, node_feat, edge_feat, w0, out):
         fold_columns(3)
         quantise_w0()
         clamp(2)
-        regroup_features(1)
         invert(2)
         for step in range(UNITS + 3):
             graph, second_step = divmod(step, CHANNELS)
@@ -416,6 +426,9 @@ def tile_nodeupdatenetwork_pa_kernel(tc, node_feat, edge_feat, w0, out):
             normalise(step + 2)
             transpose_edges(step + 2)
             interleave_features(*divmod(step + 1, HALVES))
+            fold_follows = second_step and step + 4 < UNITS
+            if fold_follows:
+                slope(graph - 1)
             if second_step:
                 quantise_x0(graph)
             quantise_aggr(step - 1)
@@ -429,12 +442,13 @@ def tile_nodeupdatenetwork_pa_kernel(tc, node_feat, edge_feat, w0, out):
             first_matmul(step + 1, range(4))
             if second_step:
                 regroup_features(graph + 2)
-                slope(graph - 1)
                 invert(step + 3)
-                clear_signs(step + 4)
-                if step + 4 < UNITS:
+                if fold_follows:
+                    clear_signs(step + 4)
                     leaky_relu_and_store(graph - 1)
                     fold_columns(step + 4)
+                else:
+                    slope(graph - 1)
             else:
                 invert(step + 3)
                 quantise_features(graph + 1)

@@ -22,8 +22,6 @@ EPS = 1e-12
 SLOPE = 0.01
 SIGN_CLEARED = 0x7FFF7FFF
 
-W0_STEP = -1
-
 FLOPS = 2 * GRAPHS * CHANNELS * NODES * NODES * FEATURES + 2 * GRAPHS * NODES * X_PASSES * FEATURES * OUT_WIDTH
 
 
@@ -79,17 +77,23 @@ def tile_nodeupdatenetwork_pa_kernel(tc, node_feat, edge_feat, w0, out):
                 in_=node_feat[t].rearrange("(u p e) d -> p u (e d)", u=2, e=2),
             )
 
-        order_of_need = [0, 2, 1, 4, 3, 5, 6, 7]
-        for t in range(GRAPHS):
-            for s in order_of_need[2 * t : 2 * t + 2]:
-                load_edges(s)
-            if t == 1:
-                nc.sync.dma_start(out=w0_rows[:], in_=w0)
-            load_features_by_pair(t)
-            if t == 0:
-                continue
-            load_rows(t - 1)
-        load_rows(GRAPHS - 1)
+        load_edges(0)
+        load_edges(1)
+        load_features_by_pair(0)
+        nc.sync.dma_start(out=w0_rows[:], in_=w0)
+        load_rows(0)
+        load_edges(2)
+        load_edges(3)
+        load_features_by_pair(1)
+        load_edges(4)
+        load_rows(1)
+        load_edges(5)
+        load_edges(6)
+        load_features_by_pair(2)
+        load_rows(2)
+        load_edges(7)
+        load_features_by_pair(3)
+        load_rows(3)
 
         ident_f32 = consts.tile([P, P], F32)
         make_identity(nc, ident_f32[:])
@@ -382,49 +386,47 @@ def tile_nodeupdatenetwork_pa_kernel(tc, node_feat, edge_feat, w0, out):
         scalar_row_sums(0, 0)
         scalar_row_sums(0, 1)
         vector_row_sums(0)
-        mask(2)
-        scalar_row_sums(2, 0)
         clamp(0)
         invert(0)
         normalise(0)
         transpose_edges(0)
-        regroup_features(0)
         mask(1)
-        quantise_features(0)
         clear_signs(1)
-        mask(4)
+        fold_columns(1)
+        regroup_features(0)
         interleave_edges(0, 0)
         interleave_edges(0, 1)
-        scalar_row_sums(2, 1)
-        scalar_row_sums(4, 0)
         transpose_w0()
         interleave_w0()
-        fold_columns(1)
+        quantise_features(0)
         quantise_edges(0)
-        regroup_features(1)
-        first_matmul(0, range(4))
-        vector_row_sums(1)
-        clamp(1)
-        mask(3)
-        invert(1)
         transpose_features(0, 0)
         interleave_features(0, 0)
-        scalar_row_sums(4, 1)
-        clear_signs(3)
+        vector_row_sums(1)
+        clamp(1)
+        mask(2)
+        scalar_row_sums(2, 0)
+        first_matmul(0, range(4))
+        invert(1)
+        quantise_w0()
         normalise(1)
         transpose_edges(1)
         transpose_features(0, 1)
+        mask(3)
+        clear_signs(3)
+        scalar_row_sums(2, 1)
         fold_columns(3)
-        quantise_w0()
         clamp(2)
         invert(2)
         for step in range(UNITS + 3):
             graph, second_step = divmod(step, CHANNELS)
             interleave_edges(step + 1, 0)
             interleave_edges(step + 1, 1)
-            mask(step + 5)
             normalise(step + 2)
             transpose_edges(step + 2)
+            mask(step + 4)
+            if step == 0:
+                regroup_features(1)
             interleave_features(*divmod(step + 1, HALVES))
             fold_follows = second_step and step + 4 < UNITS
             if fold_follows:
@@ -433,11 +435,13 @@ def tile_nodeupdatenetwork_pa_kernel(tc, node_feat, edge_feat, w0, out):
                 quantise_x0(graph)
             quantise_aggr(step - 1)
             if not second_step:
-                vector_row_sums(step + 3)
                 leaky_relu_and_store(graph - 2)
             transpose_features(*divmod(step + 2, HALVES))
             quantise_edges(step + 1)
-            clamp(step + 3)
+            if not second_step:
+                vector_row_sums(step + 3)
+            else:
+                clamp(step + 3)
             round_aggr(step, range(4))
             first_matmul(step + 1, range(4))
             if second_step:
@@ -450,9 +454,9 @@ def tile_nodeupdatenetwork_pa_kernel(tc, node_feat, edge_feat, w0, out):
                 else:
                     slope(graph - 1)
             else:
-                invert(step + 3)
                 quantise_features(graph + 1)
+                clamp(step + 3)
+                invert(step + 3)
                 second_matmul(graph - 1)
-            scalar_row_sums(step + 5, 0)
-            if step:
-                scalar_row_sums(step + 4, 1)
+            scalar_row_sums(step + 4, 0)
+            scalar_row_sums(step + 4, 1)

@@ -22,6 +22,9 @@ EPS = 1e-12
 SLOPE = 0.01
 SIGN_CLEARED = 0x7FFF7FFF
 
+FOLDED_UNITS = (3, 5, 7)
+VECTOR_TILES = {1: (3,), 4: (3,), 6: (3,), 7: (3,)}
+
 FLOPS = 2 * GRAPHS * CHANNELS * NODES * NODES * FEATURES + 2 * GRAPHS * NODES * X_PASSES * FEATURES * OUT_WIDTH
 
 
@@ -36,7 +39,7 @@ def tile_nodeupdatenetwork_pa_kernel(tc, node_feat, edge_feat, w0, out):
         edge_pool = ctx.enter_context(tc.tile_pool(name="edge_pool", bufs=UNITS))
         feat_pool = ctx.enter_context(tc.tile_pool(name="feat_pool", bufs=GRAPHS))
         work = ctx.enter_context(tc.tile_pool(name="work", bufs=2))
-        outputs = ctx.enter_context(tc.tile_pool(name="outputs", bufs=4))
+        outputs = ctx.enter_context(tc.tile_pool(name="outputs", bufs=6))
         small = ctx.enter_context(tc.tile_pool(name="small", bufs=4))
         scratch = ctx.enter_context(tc.tile_pool(name="scratch", bufs=4))
         word_psum = ctx.enter_context(tc.psum_pool(name="word_psum", bufs=3))
@@ -80,8 +83,8 @@ def tile_nodeupdatenetwork_pa_kernel(tc, node_feat, edge_feat, w0, out):
         load_edges(0)
         load_edges(1)
         load_features_by_pair(0)
-        nc.sync.dma_start(out=w0_rows[:], in_=w0)
         load_rows(0)
+        nc.sync.dma_start(out=w0_rows[:], in_=w0)
         load_edges(2)
         load_edges(3)
         load_features_by_pair(1)
@@ -124,26 +127,29 @@ def tile_nodeupdatenetwork_pa_kernel(tc, node_feat, edge_feat, w0, out):
         w0_scales = consts.tile([P, X_PASSES, OUT_WIDTH], U8, align_bytes=64)
         w0_banks = {}
 
-        def transpose_w0():
-            w0_banks[0] = word_psum.tile([P, 2, P], F32, name="bank")
-            for u in range(2):
-                nc.tensor.transpose(w0_banks[0][:, u, :], w0_rows[:].bitcast(F32)[:, u * P : (u + 1) * P], ident_f32[:])
+        def transpose_w0(g):
+            if g == 0:
+                w0_banks[0] = word_psum.tile([P, 2, P], F32, name="bank")
+                for u in range(2):
+                    nc.tensor.transpose(w0_banks[0][:, u, :], w0_rows[:].bitcast(F32)[:, u * P : (u + 1) * P], ident_f32[:])
+                return
+            w0_banks[1] = out_psum.tile([P, X_PASSES - 1, FEATURE_TILES, P], BF16, name="out_bank")
             for g in range(1, X_PASSES):
-                w0_banks[g] = word_psum.tile([P, FEATURE_TILES, P], BF16, name="bank")
                 for j in range(FEATURE_TILES):
                     first = g * FEATURES + j * P
-                    nc.tensor.transpose(w0_banks[g][:, j, :], w0_rows[:, first : first + P], ident_bf16[:])
+                    nc.tensor.transpose(w0_banks[1][:, g - 1, j, :], w0_rows[:, first : first + P], ident_bf16[:])
 
-        def interleave_w0():
-            nc.scalar.copy(
-                out=w0_grouped[:, 0, :].bitcast(F32).rearrange("p (h u) -> p h u", u=2),
-                in_=w0_banks[0][:].rearrange("p u h -> p h u"),
-            )
-            for g in range(1, X_PASSES):
+        def interleave_w0(g):
+            if g == 0:
                 nc.scalar.copy(
-                    out=w0_grouped[:, g, :].rearrange("p (h j) -> p h j", j=PACK),
-                    in_=w0_banks[g][:].rearrange("p j h -> p h j"),
+                    out=w0_grouped[:, 0, :].bitcast(F32).rearrange("p (h u) -> p h u", u=2),
+                    in_=w0_banks[0][:].rearrange("p u h -> p h u"),
                 )
+                return
+            nc.scalar.copy(
+                out=w0_grouped[:, 1:X_PASSES, :].rearrange("p g (h j) -> p g h j", j=PACK),
+                in_=w0_banks[1][:].rearrange("p g j h -> p g h j"),
+            )
 
         def quantise_w0():
             for g in range(X_PASSES):
@@ -187,22 +193,22 @@ def tile_nodeupdatenetwork_pa_kernel(tc, node_feat, edge_feat, w0, out):
             x_scales[t] = work.tile([P, X_PASSES, NODES], U8, align_bytes=64, name="x_scales")
             quantise(x0_grouped[t][:], x_codes[t][:, 0, :], x_scales[t][:, 0, :])
 
-        def second_matmul(t):
+        def second_matmul(t, passes=range(X_PASSES)):
             if t not in x_codes:
                 return
-            tiles_in_a_bank = NODE_TILES // 2 if t == GRAPHS - 1 else NODE_TILES
-            out_banks[t] = []
+            tiles_in_a_bank = 1 if t == GRAPHS - 1 else NODE_TILES
+            banks = out_banks.setdefault(t, [])
             for i in range(NODE_TILES):
                 nodes = slice(i * P, (i + 1) * P)
-                if i % tiles_in_a_bank == 0:
-                    if t == GRAPHS - 1:
+                if 0 in passes and i % tiles_in_a_bank == 0:
+                    if t == GRAPHS - 1 and i < NODE_TILES - 1:
                         out_bank = word_psum.tile([P, tiles_in_a_bank, OUT_WIDTH], F32, name="bank")
                     else:
                         out_bank = out_psum.tile([P, tiles_in_a_bank, OUT_WIDTH], F32, name="out_bank")
-                    out_banks[t].append(out_bank)
-                for g in range(X_PASSES):
+                    banks.append(out_bank)
+                for g in passes:
                     nc.tensor.matmul_mx(
-                        out=out_banks[t][-1][:, i % tiles_in_a_bank, :],
+                        out=banks[i // tiles_in_a_bank][:, i % tiles_in_a_bank, :],
                         lhsT=x_codes[t][:, g, nodes].bitcast(FP8X4),
                         lhsT_scale=x_scales[t][:, g, nodes],
                         rhs=w0_codes[:, g, :].bitcast(FP8X4),
@@ -255,7 +261,7 @@ def tile_nodeupdatenetwork_pa_kernel(tc, node_feat, edge_feat, w0, out):
             )
 
         def scalar_row_sums(s, half):
-            if s not in masked or s % CHANNELS == 1:
+            if s not in masked or s in FOLDED_UNITS:
                 return
             if half == 0:
                 denom[s] = small.tile([P, NODE_TILES], F32, name="denom")
@@ -266,7 +272,7 @@ def tile_nodeupdatenetwork_pa_kernel(tc, node_feat, edge_feat, w0, out):
                 )
 
         def clear_signs(s):
-            if s not in masked or s % CHANNELS == 0:
+            if s not in FOLDED_UNITS:
                 return
             magnitudes[s] = work.tile([P, NODE_TILES, NODES], BF16, name="magnitudes")
             nc.vector.tensor_scalar(
@@ -362,7 +368,7 @@ def tile_nodeupdatenetwork_pa_kernel(tc, node_feat, edge_feat, w0, out):
             if s not in aggr_grouped:
                 aggr_grouped[s] = work.tile([P, NODES, PACK], BF16, align_bytes=64, name="aggr_grouped")
             for i in node_tiles:
-                vectors = i % 2 == 1 if s == UNITS - 1 else s in (4, 6) and i == 3
+                vectors = i in VECTOR_TILES.get(s, ())
                 copy = nc.vector.tensor_copy if vectors else nc.scalar.copy
                 copy(
                     out=aggr_grouped[s][:, i * P : (i + 1) * P, :],
@@ -387,76 +393,87 @@ def tile_nodeupdatenetwork_pa_kernel(tc, node_feat, edge_feat, w0, out):
         scalar_row_sums(0, 1)
         vector_row_sums(0)
         clamp(0)
+        mask(1)
         invert(0)
         normalise(0)
         transpose_edges(0)
-        mask(1)
-        clear_signs(1)
-        fold_columns(1)
+        scalar_row_sums(1, 0)
         regroup_features(0)
         interleave_edges(0, 0)
         interleave_edges(0, 1)
-        transpose_w0()
-        interleave_w0()
+        scalar_row_sums(1, 1)
         quantise_features(0)
         quantise_edges(0)
+        transpose_w0(0)
         transpose_features(0, 0)
+        transpose_w0(1)
+        interleave_w0(0)
         interleave_features(0, 0)
-        vector_row_sums(1)
         clamp(1)
         mask(2)
         scalar_row_sums(2, 0)
-        first_matmul(0, range(4))
         invert(1)
-        quantise_w0()
         normalise(1)
+        mask(3)
         transpose_edges(1)
         transpose_features(0, 1)
-        mask(3)
+        first_matmul(0, range(4))
         clear_signs(3)
-        scalar_row_sums(2, 1)
+        interleave_w0(1)
         fold_columns(3)
+        scalar_row_sums(2, 1)
+        regroup_features(1)
+        quantise_w0()
         clamp(2)
         invert(2)
         for step in range(UNITS + 3):
             graph, second_step = divmod(step, CHANNELS)
             interleave_edges(step + 1, 0)
             interleave_edges(step + 1, 1)
-            normalise(step + 2)
-            transpose_edges(step + 2)
-            mask(step + 4)
-            if step == 0:
-                regroup_features(1)
-            interleave_features(*divmod(step + 1, HALVES))
             fold_follows = second_step and step + 4 < UNITS
-            if fold_follows:
-                slope(graph - 1)
             if second_step:
                 quantise_x0(graph)
+            normalise(step + 2)
+            transpose_edges(step + 2)
+            if not second_step:
+                mask(step + 4)
+            interleave_features(*divmod(step + 1, HALVES))
+            last_unit = step == UNITS - 1
+            if second_step and (fold_follows or last_unit):
+                slope(graph - 1)
             quantise_aggr(step - 1)
             if not second_step:
                 leaky_relu_and_store(graph - 2)
+            if last_unit:
+                leaky_relu_and_store(graph - 1)
             transpose_features(*divmod(step + 2, HALVES))
             quantise_edges(step + 1)
             if not second_step:
                 vector_row_sums(step + 3)
             else:
                 clamp(step + 3)
+            fold_pending = step + 3 < UNITS
+            if not second_step and not fold_pending:
+                second_matmul(graph - 1, (X_PASSES - 1,) if step == UNITS else range(X_PASSES))
             round_aggr(step, range(4))
             first_matmul(step + 1, range(4))
+            if last_unit:
+                second_matmul(graph, range(X_PASSES - 1))
             if second_step:
                 regroup_features(graph + 2)
                 invert(step + 3)
+                clear_signs(step + 4)
                 if fold_follows:
-                    clear_signs(step + 4)
                     leaky_relu_and_store(graph - 1)
-                    fold_columns(step + 4)
-                else:
+                elif not last_unit:
                     slope(graph - 1)
+                fold_columns(step + 4)
             else:
                 quantise_features(graph + 1)
                 clamp(step + 3)
+                mask(step + 5)
                 invert(step + 3)
-                second_matmul(graph - 1)
+                if fold_pending:
+                    second_matmul(graph - 1)
             scalar_row_sums(step + 4, 0)
             scalar_row_sums(step + 4, 1)

@@ -22,8 +22,10 @@ EPS = 1e-12
 SLOPE = 0.01
 SIGN_CLEARED = 0x7FFF7FFF
 
-FOLDED_UNITS = (3, 5, 7)
-VECTOR_TILES = {1: (3,), 4: (3,), 6: (3,), 7: (3,)}
+FOLDED_UNITS = (3, 4, 5, 7)
+VECTOR_TILES = {4: (3,), 6: (3,), 7: (3,)}
+SHARED_UNITS = (0,)
+TILES_IN_A_LOAD = {0: 1, 1: 2}
 
 FLOPS = 2 * GRAPHS * CHANNELS * NODES * NODES * FEATURES + 2 * GRAPHS * NODES * X_PASSES * FEATURES * OUT_WIDTH
 
@@ -60,7 +62,7 @@ def tile_nodeupdatenetwork_pa_kernel(tc, node_feat, edge_feat, w0, out):
                 return
             t, e = divmod(s, CHANNELS)
             masked[s] = edge_pool.tile([P, NODE_TILES, NODES], BF16, name="edges")
-            tiles_in_a_load = 1 if s == 0 else NODE_TILES
+            tiles_in_a_load = TILES_IN_A_LOAD.get(s, NODE_TILES)
             for i in range(0, NODE_TILES, tiles_in_a_load):
                 nc.sync.dma_start(
                     out=masked[s][:, i : i + tiles_in_a_load, :],
@@ -243,20 +245,16 @@ def tile_nodeupdatenetwork_pa_kernel(tc, node_feat, edge_feat, w0, out):
         edge_codes, edge_scales, aggr_banks, aggr_grouped = {}, {}, {}, {}
         magnitudes, folded = {}, {}
 
-        def mask(s):
+        def mask(s, first_tile=0, tiles=NODE_TILES):
             if s not in masked:
                 return
-            if s == 0:
-                for i in range(NODE_TILES):
-                    diagonal_block = masked[s][:, i, i * P : (i + 1) * P]
-                    nc.vector.tensor_tensor(out=diagonal_block, in0=diagonal_block, in1=off_diagonal[:], op=ALU.mult)
-                return
             blocks = masked[s][:].rearrange("p i (b c) -> p (i b) c", c=P)
-            diagonal_blocks = blocks[:, 0 : NODE_TILES * NODE_TILES : NODE_TILES + 1, :]
+            step_of_diagonal = NODE_TILES + 1
+            diagonal_blocks = blocks[:, first_tile * step_of_diagonal : (first_tile + tiles - 1) * step_of_diagonal + 1 : step_of_diagonal, :]
             nc.vector.tensor_tensor(
                 out=diagonal_blocks,
                 in0=diagonal_blocks,
-                in1=off_diagonal[:].unsqueeze(1).to_broadcast([P, NODE_TILES, P]),
+                in1=off_diagonal[:].unsqueeze(1).to_broadcast([P, tiles, P]),
                 op=ALU.mult,
             )
 
@@ -265,7 +263,7 @@ def tile_nodeupdatenetwork_pa_kernel(tc, node_feat, edge_feat, w0, out):
                 return
             if half == 0:
                 denom[s] = small.tile([P, NODE_TILES], F32, name="denom")
-            for i in range(2 * half, 3 if s == 0 and half == 1 else 2 * half + 2):
+            for i in range(2 * half, 3 if s in SHARED_UNITS and half == 1 else 2 * half + 2):
                 absolute = scratch.tile([P, NODES], BF16)
                 nc.scalar.activation(
                     out=absolute[:], in_=masked[s][:, i, :], func=ACT.Abs, accum_out=denom[s][:, i : i + 1]
@@ -292,7 +290,7 @@ def tile_nodeupdatenetwork_pa_kernel(tc, node_feat, edge_feat, w0, out):
                 )
 
         def vector_row_sums(s):
-            if s == 0:
+            if s in SHARED_UNITS:
                 nc.vector.tensor_reduce(
                     out=denom[s][:, 3:4], in_=masked[s][:, 3:4, :], axis=mybir.AxisListType.X, op=ALU.add,
                     apply_absolute_value=True,
@@ -388,12 +386,16 @@ def tile_nodeupdatenetwork_pa_kernel(tc, node_feat, edge_feat, w0, out):
                     x_scales[t][:, 1 + e, nodes],
                 )
 
-        mask(0)
+        mask(0, 0, 1)
+        mask(0, 1, 1)
+        mask(0, 2, 1)
+        mask(0, 3, 1)
         scalar_row_sums(0, 0)
         scalar_row_sums(0, 1)
         vector_row_sums(0)
+        mask(1, 0, 2)
         clamp(0)
-        mask(1)
+        mask(1, 2, 2)
         invert(0)
         normalise(0)
         transpose_edges(0)
@@ -426,6 +428,7 @@ def tile_nodeupdatenetwork_pa_kernel(tc, node_feat, edge_feat, w0, out):
         quantise_w0()
         clamp(2)
         invert(2)
+        mask(4)
         for step in range(UNITS + 3):
             graph, second_step = divmod(step, CHANNELS)
             interleave_edges(step + 1, 0)
@@ -435,8 +438,6 @@ def tile_nodeupdatenetwork_pa_kernel(tc, node_feat, edge_feat, w0, out):
                 quantise_x0(graph)
             normalise(step + 2)
             transpose_edges(step + 2)
-            if not second_step:
-                mask(step + 4)
             interleave_features(*divmod(step + 1, HALVES))
             last_unit = step == UNITS - 1
             if second_step and (fold_follows or last_unit):
@@ -448,10 +449,8 @@ def tile_nodeupdatenetwork_pa_kernel(tc, node_feat, edge_feat, w0, out):
                 leaky_relu_and_store(graph - 1)
             transpose_features(*divmod(step + 2, HALVES))
             quantise_edges(step + 1)
-            if not second_step:
-                vector_row_sums(step + 3)
-            else:
-                clamp(step + 3)
+            vector_row_sums(step + 3)
+            mask(step + 5)
             fold_pending = step + 3 < UNITS
             if not second_step and not fold_pending:
                 second_matmul(graph - 1, (X_PASSES - 1,) if step == UNITS else range(X_PASSES))
@@ -459,6 +458,7 @@ def tile_nodeupdatenetwork_pa_kernel(tc, node_feat, edge_feat, w0, out):
             first_matmul(step + 1, range(4))
             if last_unit:
                 second_matmul(graph, range(X_PASSES - 1))
+            clamp(step + 3)
             if second_step:
                 regroup_features(graph + 2)
                 invert(step + 3)
@@ -470,10 +470,10 @@ def tile_nodeupdatenetwork_pa_kernel(tc, node_feat, edge_feat, w0, out):
                 fold_columns(step + 4)
             else:
                 quantise_features(graph + 1)
-                clamp(step + 3)
-                mask(step + 5)
                 invert(step + 3)
                 if fold_pending:
                     second_matmul(graph - 1)
+                clear_signs(step + 4)
+                fold_columns(step + 4)
             scalar_row_sums(step + 4, 0)
             scalar_row_sums(step + 4, 1)

@@ -23,8 +23,8 @@ SLOPE = 0.01
 SIGN_CLEARED = 0x7FFF7FFF
 
 FOLDED_UNITS = (3, 4, 5, 7)
-VECTOR_TILES = {4: (3,), 6: (3,), 7: (3,)}
-SHARED_UNITS = (0,)
+VECTOR_TILES = {6: (3,), 7: (3,)}
+SHARED_UNITS = (0, 1)
 TILES_IN_A_LOAD = {0: 1, 1: 2}
 
 FLOPS = 2 * GRAPHS * CHANNELS * NODES * NODES * FEATURES + 2 * GRAPHS * NODES * X_PASSES * FEATURES * OUT_WIDTH
@@ -54,7 +54,7 @@ def tile_nodeupdatenetwork_pa_kernel(tc, node_feat, edge_feat, w0, out):
         nc.vector.memset(table_seed[:], 0.0)
         nc.scalar.activation(out=table_ready[:], in_=table_seed[:], func=ACT.Abs)
 
-        masked, feat_by_pair, feat_rows = {}, {}, {}
+        masked, feat_by_pair = {}, {}
         w0_rows = consts.tile([P, X_PASSES * FEATURES], BF16)
 
         def load_edges(s):
@@ -69,10 +69,6 @@ def tile_nodeupdatenetwork_pa_kernel(tc, node_feat, edge_feat, w0, out):
                     in_=edge_feat[t, e, i * P : (i + tiles_in_a_load) * P, :].rearrange("(i p) m -> p i m", p=P),
                 )
 
-        def load_rows(t):
-            feat_rows[t] = feat_pool.tile([P, NODE_TILES, FEATURES], BF16, name="rows")
-            nc.sync.dma_start(out=feat_rows[t][:], in_=node_feat[t].rearrange("(i p) d -> p i d", p=P))
-
         def load_features_by_pair(t):
             if t >= GRAPHS:
                 return
@@ -85,20 +81,16 @@ def tile_nodeupdatenetwork_pa_kernel(tc, node_feat, edge_feat, w0, out):
         load_edges(0)
         load_edges(1)
         load_features_by_pair(0)
-        load_rows(0)
         nc.sync.dma_start(out=w0_rows[:], in_=w0)
         load_edges(2)
         load_edges(3)
         load_features_by_pair(1)
         load_edges(4)
-        load_rows(1)
         load_edges(5)
         load_edges(6)
         load_features_by_pair(2)
-        load_rows(2)
         load_edges(7)
         load_features_by_pair(3)
-        load_rows(3)
 
         ident_f32 = consts.tile([P, P], F32)
         make_identity(nc, ident_f32[:])
@@ -153,8 +145,8 @@ def tile_nodeupdatenetwork_pa_kernel(tc, node_feat, edge_feat, w0, out):
                 in_=w0_banks[1][:].rearrange("p g j h -> p g h j"),
             )
 
-        def quantise_w0():
-            for g in range(X_PASSES):
+        def quantise_w0(passes):
+            for g in passes:
                 quantise(w0_grouped[:, g, :], w0_codes[:, g, :], w0_scales[:, g, :])
 
         feat_grouped, feat_codes, feat_scales = {}, {}, {}
@@ -178,15 +170,19 @@ def tile_nodeupdatenetwork_pa_kernel(tc, node_feat, edge_feat, w0, out):
             quantise(feat_grouped[t][:], feat_codes[t][:], feat_scales[t][:])
 
         def transpose_features(t, half):
-            if t in feat_rows:
-                feat_banks[t, half] = transpose_words(feat_rows[t], half)
+            if t in feat_by_pair:
+                feat_banks[t, half] = transpose_words(feat_by_pair[t], half)
 
         def interleave_features(t, half):
             if (t, half) not in feat_banks:
                 return
             if half == 0:
                 x0_grouped[t] = work.tile([P, PACK * NODES], BF16, align_bytes=64, name="x0_grouped")
-            interleave_words(feat_banks[t, half], x0_grouped[t][:], half, nc.scalar.copy)
+            words = x0_grouped[t][:].bitcast(F32).rearrange("p (q e u) -> p q e u", e=2, u=2)
+            nc.scalar.copy(
+                out=words[:, half * P : (half + 1) * P, :, :],
+                in_=feat_banks[t, half][:].rearrange("p u (e q) -> p q e u", e=2),
+            )
 
         def quantise_x0(t):
             if t not in x0_grouped:
@@ -401,6 +397,7 @@ def tile_nodeupdatenetwork_pa_kernel(tc, node_feat, edge_feat, w0, out):
         transpose_edges(0)
         scalar_row_sums(1, 0)
         regroup_features(0)
+        vector_row_sums(1)
         interleave_edges(0, 0)
         interleave_edges(0, 1)
         scalar_row_sums(1, 1)
@@ -420,15 +417,16 @@ def tile_nodeupdatenetwork_pa_kernel(tc, node_feat, edge_feat, w0, out):
         transpose_edges(1)
         transpose_features(0, 1)
         first_matmul(0, range(4))
+        quantise_w0((0,))
         clear_signs(3)
         interleave_w0(1)
         fold_columns(3)
         scalar_row_sums(2, 1)
         regroup_features(1)
-        quantise_w0()
+        quantise_w0((1, 2))
         clamp(2)
-        invert(2)
         mask(4)
+        invert(2)
         for step in range(UNITS + 3):
             graph, second_step = divmod(step, CHANNELS)
             interleave_edges(step + 1, 0)

@@ -23,8 +23,9 @@ SLOPE = 0.01
 SIGN_CLEARED = 0x7FFF7FFF
 
 FOLDED_UNITS = (3, 4, 5, 7)
-VECTOR_TILES = {6: (3,), 7: (3,)}
-SHARED_UNITS = (0, 1)
+VECTOR_TILES = {4: (3,), 6: (3,), 7: (3,)}
+SHARED_UNITS = {0: 1}
+GPSIMD_UNITS = ()
 TILES_IN_A_LOAD = {0: 1, 1: 2}
 
 FLOPS = 2 * GRAPHS * CHANNELS * NODES * NODES * FEATURES + 2 * GRAPHS * NODES * X_PASSES * FEATURES * OUT_WIDTH
@@ -259,7 +260,7 @@ def tile_nodeupdatenetwork_pa_kernel(tc, node_feat, edge_feat, w0, out):
                 return
             if half == 0:
                 denom[s] = small.tile([P, NODE_TILES], F32, name="denom")
-            for i in range(2 * half, 3 if s in SHARED_UNITS and half == 1 else 2 * half + 2):
+            for i in [i for i in range(2 * half, 2 * half + 2) if i != SHARED_UNITS.get(s)]:
                 absolute = scratch.tile([P, NODES], BF16)
                 nc.scalar.activation(
                     out=absolute[:], in_=masked[s][:, i, :], func=ACT.Abs, accum_out=denom[s][:, i : i + 1]
@@ -288,7 +289,7 @@ def tile_nodeupdatenetwork_pa_kernel(tc, node_feat, edge_feat, w0, out):
         def vector_row_sums(s):
             if s in SHARED_UNITS:
                 nc.vector.tensor_reduce(
-                    out=denom[s][:, 3:4], in_=masked[s][:, 3:4, :], axis=mybir.AxisListType.X, op=ALU.add,
+                    out=denom[s][:, SHARED_UNITS[s] : SHARED_UNITS[s] + 1], in_=masked[s][:, SHARED_UNITS[s] : SHARED_UNITS[s] + 1, :], axis=mybir.AxisListType.X, op=ALU.add,
                     apply_absolute_value=True,
                 )
                 return
@@ -297,28 +298,31 @@ def tile_nodeupdatenetwork_pa_kernel(tc, node_feat, edge_feat, w0, out):
             denom[s] = small.tile([P, NODE_TILES], F32, name="denom")
             nc.vector.tensor_reduce(out=denom[s][:], in_=folded[s][:], axis=mybir.AxisListType.X, op=ALU.add)
 
-        def clamp(s):
+        def clamp(s, tiles=slice(0, NODE_TILES)):
             if s in denom:
-                inverse[s] = small.tile([P, NODE_TILES], F32, name="inverse")
-                nc.vector.tensor_scalar_max(out=inverse[s][:], in0=denom[s][:], scalar1=EPS)
+                if s not in inverse:
+                    inverse[s] = small.tile([P, NODE_TILES], F32, name="inverse")
+                engine = nc.gpsimd if s in GPSIMD_UNITS else nc.vector
+                engine.tensor_scalar_max(out=inverse[s][:, tiles], in0=denom[s][:, tiles], scalar1=EPS)
 
-        def invert(s):
+        def invert(s, tiles=slice(0, NODE_TILES)):
             if s in inverse:
-                nc.vector.reciprocal(out=inverse[s][:], in_=inverse[s][:])
+                nc.vector.reciprocal(out=inverse[s][:, tiles], in_=inverse[s][:, tiles])
 
-        def normalise(s):
+        def normalise(s, tiles=range(NODE_TILES)):
             if s not in inverse:
                 return
-            norm_edge[s] = work.tile([P, NODE_TILES, NODES], BF16, name="norm_edge")
-            for i in range(NODE_TILES):
+            if s not in norm_edge:
+                norm_edge[s] = work.tile([P, NODE_TILES, NODES], BF16, name="norm_edge")
+            for i in tiles:
                 nc.vector.tensor_scalar(
                     out=norm_edge[s][:, i, :], in0=masked[s][:, i, :], scalar1=inverse[s][:, i : i + 1], scalar2=None,
                     op0=ALU.mult,
                 )
 
-        def transpose_edges(s):
+        def transpose_edges(s, halves=range(HALVES)):
             if s in norm_edge:
-                edge_banks[s] = [transpose_words(norm_edge[s], half) for half in range(HALVES)]
+                edge_banks.setdefault(s, []).extend([transpose_words(norm_edge[s], half) for half in halves])
 
         def interleave_edges(s, half):
             if s not in edge_banks:
@@ -385,19 +389,22 @@ def tile_nodeupdatenetwork_pa_kernel(tc, node_feat, edge_feat, w0, out):
         mask(0, 0, 1)
         mask(0, 1, 1)
         mask(0, 2, 1)
-        mask(0, 3, 1)
         scalar_row_sums(0, 0)
-        scalar_row_sums(0, 1)
         vector_row_sums(0)
+        mask(0, 3, 1)
+        clamp(0, slice(0, 2))
+        scalar_row_sums(0, 1)
         mask(1, 0, 2)
-        clamp(0)
+        invert(0, slice(0, 2))
+        clamp(0, slice(2, 4))
+        normalise(0, range(2))
+        transpose_edges(0, range(1))
+        invert(0, slice(2, 4))
         mask(1, 2, 2)
-        invert(0)
-        normalise(0)
-        transpose_edges(0)
+        normalise(0, range(2, 4))
+        transpose_edges(0, range(1, 2))
         scalar_row_sums(1, 0)
         regroup_features(0)
-        vector_row_sums(1)
         interleave_edges(0, 0)
         interleave_edges(0, 1)
         scalar_row_sums(1, 1)

@@ -23,9 +23,10 @@ SLOPE = 0.01
 SIGN_CLEARED = 0x7FFF7FFF
 
 FOLDED_UNITS = (3, 4, 5, 7)
-VECTOR_TILES = {4: (3,), 6: (3,), 7: (3,)}
+VECTOR_TILES = {4: (3,), 5:(3,),6: (3,), 7: (3,)}
 SHARED_UNITS = {0: 1}
 GPSIMD_UNITS = ()
+FOLD_WIDTH = 32
 TILES_IN_A_LOAD = {0: 1, 1: 2}
 
 FLOPS = 2 * GRAPHS * CHANNELS * NODES * NODES * FEATURES + 2 * GRAPHS * NODES * X_PASSES * FEATURES * OUT_WIDTH
@@ -279,11 +280,11 @@ def tile_nodeupdatenetwork_pa_kernel(tc, node_feat, edge_feat, w0, out):
         def fold_columns(s):
             if s not in magnitudes:
                 return
-            folded[s] = out_psum.tile([P, NODE_TILES, P], F32, name="out_bank")
-            for b in range(NODES // P):
+            folded[s] = out_psum.tile([P, NODE_TILES, FOLD_WIDTH], F32, name="out_bank")
+            for b in range(NODES // FOLD_WIDTH):
                 nc.tensor.matmul(
-                    out=folded[s][:], lhsT=ident_bf16[:], rhs=magnitudes[s][:, :, b * P : (b + 1) * P],
-                    start=(b == 0), stop=(b == NODES // P - 1),
+                    out=folded[s][:], lhsT=ident_bf16[:], rhs=magnitudes[s][:, :, b * FOLD_WIDTH : (b + 1) * FOLD_WIDTH],
+                    start=(b == 0), stop=(b == NODES // FOLD_WIDTH - 1),
                 )
 
         def vector_row_sums(s):

@@ -23,7 +23,7 @@ SLOPE = 0.01
 SIGN_CLEARED = 0x7FFF7FFF
 
 FOLDED_UNITS = (3, 4, 5, 7)
-VECTOR_TILES = {4: (3,), 5:(3,),6: (3,), 7: (3,)}
+VECTOR_TILES = {5:(3,),6:(3,),7:(3,)}
 SHARED_UNITS = {0: 1}
 GPSIMD_UNITS = ()
 FOLD_WIDTH = 32
@@ -148,8 +148,11 @@ def tile_nodeupdatenetwork_pa_kernel(tc, node_feat, edge_feat, w0, out):
             )
 
         def quantise_w0(passes):
-            for g in passes:
-                quantise(w0_grouped[:, g, :], w0_codes[:, g, :], w0_scales[:, g, :])
+            quantise(
+                w0_grouped[:, passes, :].rearrange("p g k -> p (g k)"),
+                w0_codes[:, passes, :].rearrange("p g h -> p (g h)"),
+                w0_scales[:, passes, :].rearrange("p g h -> p (g h)"),
+            )
 
         feat_grouped, feat_codes, feat_scales = {}, {}, {}
         feat_banks, x0_grouped, x_codes, x_scales = {}, {}, {}, {}
@@ -425,13 +428,13 @@ def tile_nodeupdatenetwork_pa_kernel(tc, node_feat, edge_feat, w0, out):
         transpose_edges(1)
         transpose_features(0, 1)
         first_matmul(0, range(4))
-        quantise_w0((0,))
+        quantise_w0(slice(0, 1))
         clear_signs(3)
         interleave_w0(1)
         fold_columns(3)
         scalar_row_sums(2, 1)
         regroup_features(1)
-        quantise_w0((1, 2))
+        quantise_w0(slice(1, X_PASSES))
         clamp(2)
         mask(4)
         invert(2)

from contextlib import ExitStack

import concourse.mybir as mybir
from concourse.masks import make_identity

F32 = mybir.dt.float32
BF16 = mybir.dt.bfloat16
U32 = mybir.dt.uint32
I32 = mybir.dt.int32
U8 = mybir.dt.uint8
FP8X4 = mybir.dt.float8_e4m3fn_x4
ALU = mybir.AluOpType
ACT = mybir.ActivationFunctionType

P = 128
PACK = 4
GRAPHS, CHANNELS, NODES, FEATURES, OUT_WIDTH = 4, 2, 512, 512, 128
NODE_TILES = NODES // P
FEATURE_TILES = FEATURES // P
X_PASSES = 1 + CHANNELS
EPS = 1e-12
SLOPE = 0.01
SIGN_CLEARED = 0x7FFF7FFF

FOLDED_UNITS = (3, 4, 5, 7)
VECTOR_TILES = {5:(3,),6:(3,),7:(3,)}
SHARED_UNITS = {0: 1}
GPSIMD_UNITS = ()
FOLD_WIDTH = 32
TILES_IN_A_LOAD = {0: 1, 1: 2}

FLOPS = 2 * GRAPHS * CHANNELS * NODES * NODES * FEATURES + 2 * GRAPHS * NODES * X_PASSES * FEATURES * OUT_WIDTH


UNITS = GRAPHS * CHANNELS
HALVES = 2


def tile_nodeupdatenetwork_pa_kernel(tc, node_feat, edge_feat, w0, out):
    nc = tc.nc
    with ExitStack() as ctx:
        consts = ctx.enter_context(tc.tile_pool(name="consts", bufs=1))
        edge_pool = ctx.enter_context(tc.tile_pool(name="edge_pool", bufs=UNITS))
        feat_pool = ctx.enter_context(tc.tile_pool(name="feat_pool", bufs=GRAPHS))
        work = ctx.enter_context(tc.tile_pool(name="work", bufs=2))
        outputs = ctx.enter_context(tc.tile_pool(name="outputs", bufs=6))
        small = ctx.enter_context(tc.tile_pool(name="small", bufs=4))
        scratch = ctx.enter_context(tc.tile_pool(name="scratch", bufs=4))
        word_psum = ctx.enter_context(tc.psum_pool(name="word_psum", bufs=3))
        aggr_psum = ctx.enter_context(tc.psum_pool(name="aggr_psum", bufs=NODE_TILES))
        out_psum = ctx.enter_context(tc.psum_pool(name="out_psum", bufs=1))
        ctx.enter_context(tc.manual_schedule())

        table_seed = consts.tile([P, 1], F32)
        table_ready = consts.tile([P, 1], F32)
        nc.vector.memset(table_seed[:], 0.0)
        nc.scalar.activation(out=table_ready[:], in_=table_seed[:], func=ACT.Abs)

        masked, feat_by_pair = {}, {}
        w0_rows = consts.tile([P, X_PASSES * FEATURES], BF16)

        def load_edges(s):
            if s >= UNITS:
                return
            t, e = divmod(s, CHANNELS)
            masked[s] = edge_pool.tile([P, NODE_TILES, NODES], BF16, name="edges")
            tiles_in_a_load = TILES_IN_A_LOAD.get(s, NODE_TILES)
            for i in range(0, NODE_TILES, tiles_in_a_load):
                nc.sync.dma_start(
                    out=masked[s][:, i : i + tiles_in_a_load, :],
                    in_=edge_feat[t, e, i * P : (i + tiles_in_a_load) * P, :].rearrange("(i p) m -> p i m", p=P),
                )

        def load_features_by_pair(t):
            if t >= GRAPHS:
                return
            feat_by_pair[t] = feat_pool.tile([P, PACK, FEATURES], BF16, name="by_pair")
            nc.sync.dma_start(
                out=feat_by_pair[t][:].rearrange("p (u e) d -> p u (e d)", u=2),
                in_=node_feat[t].rearrange("(u p e) d -> p u (e d)", u=2, e=2),
            )

        load_edges(0)
        load_edges(1)
        load_features_by_pair(0)
        nc.sync.dma_start(out=w0_rows[:], in_=w0)
        load_edges(2)
        load_edges(3)
        load_features_by_pair(1)
        load_edges(4)
        load_edges(5)
        load_edges(6)
        load_features_by_pair(2)
        load_edges(7)
        load_features_by_pair(3)

        ident_f32 = consts.tile([P, P], F32)
        make_identity(nc, ident_f32[:])
        ident_bf16 = consts.tile([P, P], BF16)
        make_identity(nc, ident_bf16[:])
        off_diagonal = consts.tile([P, P], BF16)
        nc.vector.tensor_scalar(
            out=off_diagonal[:], in0=ident_bf16[:], scalar1=-1.0, scalar2=1.0, op0=ALU.mult, op1=ALU.add
        )

        def quantise(grouped, codes, scales):
            nc.vector.quantize_mx(out=codes.bitcast(FP8X4), scales=scales, in_=grouped)

        def transpose_words(matrix_rows, half):
            bank = word_psum.tile([P, 2, HALVES * P], F32, name="bank")
            for i in range(2):
                row_words = matrix_rows[:, 2 * half + i, :].bitcast(F32)
                for u in range(2):
                    nc.tensor.transpose(bank[:, u, i * P : (i + 1) * P], row_words[:, u * P : (u + 1) * P], ident_f32[:])
            return bank

        def interleave_words(bank, grouped, half, copy):
            words = grouped.bitcast(F32).rearrange("p (r u) -> p r u", u=2)
            copy(out=words[:, half * 2 * P : (half + 1) * 2 * P, :], in_=bank[:].rearrange("p u r -> p r u"))

        w0_grouped = consts.tile([P, X_PASSES, PACK * OUT_WIDTH], BF16, align_bytes=64)
        w0_codes = consts.tile([P, X_PASSES, OUT_WIDTH], U32, align_bytes=64)
        w0_scales = consts.tile([P, X_PASSES, OUT_WIDTH], U8, align_bytes=64)
        w0_banks = {}

        def transpose_w0(g):
            if g == 0:
                w0_banks[0] = word_psum.tile([P, 2, P], F32, name="bank")
                for u in range(2):
                    nc.tensor.transpose(w0_banks[0][:, u, :], w0_rows[:].bitcast(F32)[:, u * P : (u + 1) * P], ident_f32[:])
                return
            w0_banks[1] = out_psum.tile([P, X_PASSES - 1, FEATURE_TILES, P], BF16, name="out_bank")
            for g in range(1, X_PASSES):
                for j in range(FEATURE_TILES):
                    first = g * FEATURES + j * P
                    nc.tensor.transpose(w0_banks[1][:, g - 1, j, :], w0_rows[:, first : first + P], ident_bf16[:])

        def interleave_w0(g):
            if g == 0:
                nc.scalar.copy(
                    out=w0_grouped[:, 0, :].bitcast(F32).rearrange("p (h u) -> p h u", u=2),
                    in_=w0_banks[0][:].rearrange("p u h -> p h u"),
                )
                return
            nc.scalar.copy(
                out=w0_grouped[:, 1:X_PASSES, :].rearrange("p g (h j) -> p g h j", j=PACK),
                in_=w0_banks[1][:].rearrange("p g j h -> p g h j"),
            )

        def quantise_w0(passes):
            quantise(
                w0_grouped[:, passes, :].rearrange("p g k -> p (g k)"),
                w0_codes[:, passes, :].rearrange("p g h -> p (g h)"),
                w0_scales[:, passes, :].rearrange("p g h -> p (g h)"),
            )

        feat_grouped, feat_codes, feat_scales = {}, {}, {}
        feat_banks, x0_grouped, x_codes, x_scales = {}, {}, {}, {}
        out_banks, sloped = {}, {}

        def regroup_features(t):
            if t not in feat_by_pair:
                return
            feat_grouped[t] = work.tile([P, PACK * FEATURES], BF16, align_bytes=64, name="feat_grouped")
            nc.vector.tensor_copy(
                out=feat_grouped[t][:].rearrange("p (c i v) -> p c v i", i=4, v=PACK),
                in_=feat_by_pair[t][:].rearrange("p v (c i) -> p c v i", i=4),
            )

        def quantise_features(t):
            if t not in feat_grouped:
                return
            feat_codes[t] = work.tile([P, FEATURES], U32, align_bytes=64, name="feat_codes")
            feat_scales[t] = work.tile([P, FEATURES], U8, align_bytes=64, name="feat_scales")
            quantise(feat_grouped[t][:], feat_codes[t][:], feat_scales[t][:])

        def transpose_features(t, half):
            if t in feat_by_pair:
                feat_banks[t, half] = transpose_words(feat_by_pair[t], half)

        def interleave_features(t, half):
            if (t, half) not in feat_banks:
                return
            if half == 0:
                x0_grouped[t] = work.tile([P, PACK * NODES], BF16, align_bytes=64, name="x0_grouped")
            words = x0_grouped[t][:].bitcast(F32).rearrange("p (q e u) -> p q e u", e=2, u=2)
            nc.scalar.copy(
                out=words[:, half * P : (half + 1) * P, :, :],
                in_=feat_banks[t, half][:].rearrange("p u (e q) -> p q e u", e=2),
            )

        def quantise_x0(t):
            if t not in x0_grouped:
                return
            x_codes[t] = work.tile([P, X_PASSES, NODES], U32, align_bytes=64, name="x_codes")
            x_scales[t] = work.tile([P, X_PASSES, NODES], U8, align_bytes=64, name="x_scales")
            quantise(x0_grouped[t][:], x_codes[t][:, 0, :], x_scales[t][:, 0, :])

        def second_matmul(t, passes=range(X_PASSES)):
            if t not in x_codes:
                return
            tiles_in_a_bank = 1 if t == GRAPHS - 1 else NODE_TILES
            banks = out_banks.setdefault(t, [])
            for i in range(NODE_TILES):
                nodes = slice(i * P, (i + 1) * P)
                if 0 in passes and i % tiles_in_a_bank == 0:
                    if t == GRAPHS - 1 and i < NODE_TILES - 1:
                        out_bank = word_psum.tile([P, tiles_in_a_bank, OUT_WIDTH], F32, name="bank")
                    else:
                        out_bank = out_psum.tile([P, tiles_in_a_bank, OUT_WIDTH], F32, name="out_bank")
                    banks.append(out_bank)
                for g in passes:
                    nc.tensor.matmul_mx(
                        out=banks[i // tiles_in_a_bank][:, i % tiles_in_a_bank, :],
                        lhsT=x_codes[t][:, g, nodes].bitcast(FP8X4),
                        lhsT_scale=x_scales[t][:, g, nodes],
                        rhs=w0_codes[:, g, :].bitcast(FP8X4),
                        rhs_scale=w0_scales[:, g, :],
                        start=(g == 0),
                        stop=(g == X_PASSES - 1),
                    )

        def slope(t):
            if t not in out_banks:
                return
            sloped[t] = []
            for bank in out_banks[t]:
                times_slope = outputs.tile(bank.shape, F32, name="times_slope")
                nc.scalar.activation(out=times_slope[:], in_=bank[:], func=ACT.Copy, scale=SLOPE)
                sloped[t].append(times_slope)

        def leaky_relu_and_store(t):
            if t not in sloped:
                return
            first_row = 0
            for bank, times_slope in zip(out_banks[t], sloped.pop(t)):
                result = outputs.tile(bank.shape, F32, name="result")
                nc.vector.tensor_tensor(out=result[:], in0=bank[:], in1=times_slope[:], op=ALU.max)
                end_row = first_row + bank.shape[1] * P
                nc.sync.dma_start(
                    out=out[t, first_row:end_row, :].rearrange("(i p) h -> p i h", p=P), in_=result[:]
                )
                first_row = end_row

        denom, inverse, norm_edge, edge_banks, edge_grouped = {}, {}, {}, {}, {}
        edge_codes, edge_scales, aggr_banks, aggr_grouped = {}, {}, {}, {}
        magnitudes, folded = {}, {}

        def mask(s, first_tile=0, tiles=NODE_TILES):
            if s not in masked:
                return
            blocks = masked[s][:].rearrange("p i (b c) -> p (i b) c", c=P)
            step_of_diagonal = NODE_TILES + 1
            diagonal_blocks = blocks[:, first_tile * step_of_diagonal : (first_tile + tiles - 1) * step_of_diagonal + 1 : step_of_diagonal, :]
            nc.vector.tensor_tensor(
                out=diagonal_blocks,
                in0=diagonal_blocks,
                in1=off_diagonal[:].unsqueeze(1).to_broadcast([P, tiles, P]),
                op=ALU.mult,
            )

        def scalar_row_sums(s, half):
            if s not in masked or s in FOLDED_UNITS:
                return
            if half == 0:
                denom[s] = small.tile([P, NODE_TILES], F32, name="denom")
            for i in [i for i in range(2 * half, 2 * half + 2) if i != SHARED_UNITS.get(s)]:
                absolute = scratch.tile([P, NODES], BF16)
                nc.scalar.activation(
                    out=absolute[:], in_=masked[s][:, i, :], func=ACT.Abs, accum_out=denom[s][:, i : i + 1]
                )

        def clear_signs(s):
            if s not in FOLDED_UNITS:
                return
            magnitudes[s] = work.tile([P, NODE_TILES, NODES], BF16, name="magnitudes")
            nc.vector.tensor_scalar(
                out=magnitudes[s][:].rearrange("p i m -> p (i m)").bitcast(I32),
                in0=masked[s][:].rearrange("p i m -> p (i m)").bitcast(I32),
                scalar1=SIGN_CLEARED, scalar2=None, op0=ALU.bitwise_and,
            )

        def fold_columns(s):
            if s not in magnitudes:
                return
            folded[s] = out_psum.tile([P, NODE_TILES, FOLD_WIDTH], F32, name="out_bank")
            for b in range(NODES // FOLD_WIDTH):
                nc.tensor.matmul(
                    out=folded[s][:], lhsT=ident_bf16[:], rhs=magnitudes[s][:, :, b * FOLD_WIDTH : (b + 1) * FOLD_WIDTH],
                    start=(b == 0), stop=(b == NODES // FOLD_WIDTH - 1),
                )

        def vector_row_sums(s):
            if s in SHARED_UNITS:
                nc.vector.tensor_reduce(
                    out=denom[s][:, SHARED_UNITS[s] : SHARED_UNITS[s] + 1], in_=masked[s][:, SHARED_UNITS[s] : SHARED_UNITS[s] + 1, :], axis=mybir.AxisListType.X, op=ALU.add,
                    apply_absolute_value=True,
                )
                return
            if s not in folded:
                return
            denom[s] = small.tile([P, NODE_TILES], F32, name="denom")
            nc.vector.tensor_reduce(out=denom[s][:], in_=folded[s][:], axis=mybir.AxisListType.X, op=ALU.add)

        def clamp(s, tiles=slice(0, NODE_TILES)):
            if s in denom:
                if s not in inverse:
                    inverse[s] = small.tile([P, NODE_TILES], F32, name="inverse")
                engine = nc.gpsimd if s in GPSIMD_UNITS else nc.vector
                engine.tensor_scalar_max(out=inverse[s][:, tiles], in0=denom[s][:, tiles], scalar1=EPS)

        def invert(s, tiles=slice(0, NODE_TILES)):
            if s in inverse:
                nc.vector.reciprocal(out=inverse[s][:, tiles], in_=inverse[s][:, tiles])

        def normalise(s, tiles=range(NODE_TILES)):
            if s not in inverse:
                return
            if s not in norm_edge:
                norm_edge[s] = work.tile([P, NODE_TILES, NODES], BF16, name="norm_edge")
            for i in tiles:
                nc.vector.tensor_scalar(
                    out=norm_edge[s][:, i, :], in0=masked[s][:, i, :], scalar1=inverse[s][:, i : i + 1], scalar2=None,
                    op0=ALU.mult,
                )

        def transpose_edges(s, halves=range(HALVES)):
            if s in norm_edge:
                edge_banks.setdefault(s, []).extend([transpose_words(norm_edge[s], half) for half in halves])

        def interleave_edges(s, half):
            if s not in edge_banks:
                return
            if half == 0:
                edge_grouped[s] = work.tile([P, PACK * NODES], BF16, align_bytes=64, name="edge_grouped")
            copy = nc.vector.tensor_copy if half == 1 and s % CHANNELS == 1 else nc.scalar.copy
            interleave_words(edge_banks[s][half], edge_grouped[s][:], half, copy)

        def quantise_edges(s):
            if s not in edge_grouped:
                return
            edge_codes[s] = work.tile([P, NODES], U32, align_bytes=64, name="edge_codes")
            edge_scales[s] = work.tile([P, NODES], U8, align_bytes=64, name="edge_scales")
            quantise(edge_grouped[s][:], edge_codes[s][:], edge_scales[s][:])

        def first_matmul(s, node_tiles):
            if s not in edge_codes:
                return
            t = s // CHANNELS
            aggr_banks.setdefault(s, [])
            for i in node_tiles:
                nodes = slice(i * P, (i + 1) * P)
                aggr_bank = aggr_psum.tile([P, FEATURE_TILES, P], F32)
                for j in range(FEATURE_TILES):
                    features = slice(j * P, (j + 1) * P)
                    nc.tensor.matmul_mx(
                        out=aggr_bank[:, j, :],
                        lhsT=feat_codes[t][:, features].bitcast(FP8X4),
                        lhsT_scale=feat_scales[t][:, features],
                        rhs=edge_codes[s][:, nodes].bitcast(FP8X4),
                        rhs_scale=edge_scales[s][:, nodes],
                        start=True,
                        stop=True,
                    )
                aggr_banks[s].append(aggr_bank)

        def round_aggr(s, node_tiles):
            if s not in aggr_banks:
                return
            if s not in aggr_grouped:
                aggr_grouped[s] = work.tile([P, NODES, PACK], BF16, align_bytes=64, name="aggr_grouped")
            for i in node_tiles:
                vectors = i in VECTOR_TILES.get(s, ())
                copy = nc.vector.tensor_copy if vectors else nc.scalar.copy
                copy(
                    out=aggr_grouped[s][:, i * P : (i + 1) * P, :],
                    in_=aggr_banks[s][i][:].rearrange("p j n -> p n j"),
                )

        def quantise_aggr(s):
            if s not in aggr_grouped:
                return
            t, e = divmod(s, CHANNELS)
            width = P if s == UNITS - 1 else NODES
            for first in range(0, NODES, width):
                nodes = slice(first, first + width)
                quantise(
                    aggr_grouped[s][:, nodes, :].rearrange("p n j -> p (n j)"),
                    x_codes[t][:, 1 + e, nodes],
                    x_scales[t][:, 1 + e, nodes],
                )

        mask(0, 0, 1)
        mask(0, 1, 1)
        mask(0, 2, 1)
        scalar_row_sums(0, 0)
        vector_row_sums(0)
        mask(0, 3, 1)
        clamp(0, slice(0, 2))
        scalar_row_sums(0, 1)
        mask(1, 0, 2)
        invert(0, slice(0, 2))
        clamp(0, slice(2, 4))
        normalise(0, range(2))
        transpose_edges(0, range(1))
        invert(0, slice(2, 4))
        mask(1, 2, 2)
        normalise(0, range(2, 4))
        transpose_edges(0, range(1, 2))
        scalar_row_sums(1, 0)
        regroup_features(0)
        interleave_edges(0, 0)
        interleave_edges(0, 1)
        scalar_row_sums(1, 1)
        quantise_features(0)
        quantise_edges(0)
        transpose_w0(0)
        transpose_features(0, 0)
        transpose_w0(1)
        interleave_w0(0)
        interleave_features(0, 0)
        clamp(1)
        mask(2)
        scalar_row_sums(2, 0)
        invert(1)
        normalise(1)
        mask(3)
        transpose_edges(1)
        transpose_features(0, 1)
        first_matmul(0, range(4))
        quantise_w0(slice(0, 1))
        clear_signs(3)
        interleave_w0(1)
        fold_columns(3)
        scalar_row_sums(2, 1)
        regroup_features(1)
        quantise_w0(slice(1, X_PASSES))
        clamp(2)
        mask(4)
        invert(2)
        for step in range(UNITS + 3):
            graph, second_step = divmod(step, CHANNELS)
            interleave_edges(step + 1, 0)
            interleave_edges(step + 1, 1)
            fold_follows = second_step and step + 4 < UNITS
            if second_step:
                quantise_x0(graph)
            normalise(step + 2)
            transpose_edges(step + 2)
            interleave_features(*divmod(step + 1, HALVES))
            last_unit = step == UNITS - 1
            if second_step and (fold_follows or last_unit):
                slope(graph - 1)
            quantise_aggr(step - 1)
            if not second_step:
                leaky_relu_and_store(graph - 2)
            if last_unit:
                leaky_relu_and_store(graph - 1)
            transpose_features(*divmod(step + 2, HALVES))
            quantise_edges(step + 1)
            vector_row_sums(step + 3)
            mask(step + 5)
            fold_pending = step + 3 < UNITS
            if not second_step and not fold_pending:
                second_matmul(graph - 1, (X_PASSES - 1,) if step == UNITS else range(X_PASSES))
            round_aggr(step, range(4))
            first_matmul(step + 1, range(4))
            if last_unit:
                second_matmul(graph, range(X_PASSES - 1))
            clamp(step + 3)
            if second_step:
                regroup_features(graph + 2)
                invert(step + 3)
                clear_signs(step + 4)
                if fold_follows:
                    leaky_relu_and_store(graph - 1)
                elif not last_unit:
                    slope(graph - 1)
                fold_columns(step + 4)
            else:
                quantise_features(graph + 1)
                invert(step + 3)
                if fold_pending:
                    second_matmul(graph - 1)
                clear_signs(step + 4)
                fold_columns(step + 4)
            scalar_row_sums(step + 4, 0)
            scalar_row_sums(step + 4, 1)
